import numpy as np
import ml_dtypes


def mxq(x, axis, fmt="e4m3"):
    dtype, down = {"e4m3": (ml_dtypes.float8_e4m3fn, 7), "e5m2": (ml_dtypes.float8_e5m2, 14)}[fmt]
    v = np.moveaxis(np.asarray(x, np.float32).astype(ml_dtypes.bfloat16).astype(np.float64), axis, -1)
    blocks = v.reshape(v.shape[:-1] + (-1, 32))
    amax = np.abs(blocks).max(-1, keepdims=True)
    byte = np.maximum(np.where(amax > 0, np.frexp(amax)[1] - 1 + 127, 0) - down, 1)
    scale = np.exp2(byte - 127.0)
    codes = (blocks / scale).astype(np.float32).astype(dtype).astype(np.float64)
    return np.moveaxis((codes * scale).reshape(v.shape), -1, axis)


WIDE = False


def mx_kscale(k):
    if not WIDE:
        return np.ones(k)
    levels = np.array([10, -10, 5, -5, 0])
    if k % 512:
        return np.exp2(np.random.permutation(np.resize(levels, k // 32))).repeat(32)
    a = np.empty((k // 512, 16))
    for p in range(k // 512):
        a[p, :8] = np.random.permutation(np.resize(levels, 8))
        for g in range(8):
            far = levels[np.abs(levels - a[p, g]) >= 10]
            a[p, g + 8] = far[np.random.randint(len(far))]
    return np.exp2(a.ravel()).repeat(32)


BF16 = ml_dtypes.bfloat16


def bf(x):
    return np.asarray(x, np.float32).astype(BF16)


def f64(x):
    return np.asarray(x).astype(np.float64)


E2M1 = np.array([0.0, 0.5, 1.0, 1.5, 2.0, 3.0, 4.0, 6.0, -0.0, -0.5, -1.0, -1.5, -2.0, -3.0, -4.0, -6.0])


def pack_weight(w, fmt):
    k, n = w.shape
    w = f64(bf(w)).reshape(k // 32, 32, n)
    amax = np.abs(w).max(1)
    if fmt == "e4m3":
        byte = np.frexp(amax)[1] - 1 + 127 - 7
    else:
        mant, ex = np.frexp(amax / 6.0)
        byte = np.where(mant > 0.5, ex, ex - 1) + 127
    byte = np.clip(np.where(amax > 0, byte, 1), 1, 254)
    scaled = (w * np.exp2(127.0 - byte)[:, None, :]).reshape(k, n).astype(np.float32)
    by_word = np.ascontiguousarray(scaled.reshape(k // 512, 128, 4, n).transpose(0, 1, 3, 2))
    if fmt == "e4m3":
        words = by_word.astype(ml_dtypes.float8_e4m3fn).view(np.uint8)
    else:
        c = by_word.astype(ml_dtypes.float4_e2m1fn).view(np.uint8) & 0xF
        words = c[..., 0::2] | (c[..., 1::2] << 4)
    return np.ascontiguousarray(words), np.ascontiguousarray(byte.astype(np.uint8).reshape(k // 512, 16, n))


def unpack_weight(words, scales, fmt):
    g, p, n, _ = words.shape
    if fmt == "e4m3":
        vals = np.ascontiguousarray(words).view(ml_dtypes.float8_e4m3fn).astype(np.float64)
    else:
        nib = np.empty((g, p, n, 4), np.uint8)
        nib[..., 0::2] = words & 0xF
        nib[..., 1::2] = words >> 4
        vals = E2M1[nib]
    vals = vals * np.repeat(np.exp2(scales.astype(np.float64) - 127.0), 8, axis=1)[..., None]
    return vals.transpose(0, 1, 3, 2).reshape(g * 512, n)
def pack4(w):
    words, scales = pack_weight(w, "e2m1")
    return words.reshape(words.shape[0], 128, -1), scales


def unpack4(words, scales):
    return unpack_weight(words.reshape(words.shape[0], 128, -1, 2), scales, "e2m1")


B, L, C, KS, NL, BH, R = 1, 128, 512, 4, 24, 64, 4
OUT = 2 * BH * NL


def draw0():
    s, t = mx_kscale(C), mx_kscale(C)
    local_features = bf(np.random.standard_normal((B, L, C)) * s)
    wt = bf(np.random.standard_normal((C, C, KS)) / np.sqrt(C) / s[:, None, None] * t[None, :, None])
    bt = bf(np.random.standard_normal(C) * 0.5 * t)
    w1 = np.random.standard_normal((OUT, C)) / np.sqrt(C) / t[None, :]
    w1_words, w1_scales = pack4(np.ascontiguousarray(w1.T))
    return {"local_features": local_features,
            "wt": wt,
            "bt": bt,
            "w1_words": w1_words,
            "w1_scales": w1_scales,
            "b1": bf(np.random.standard_normal(OUT) * 0.5)}


def core(local_features, wt, bt, w1_words, w1_scales, b1):
    xq = mxq(f64(local_features), 2, "e4m3")
    wq = mxq(f64(wt), 0, "e4m3")
    up = xq @ wq.reshape(C, C * KS)
    up = up.reshape(B, L, C, KS).transpose(0, 2, 1, 3).reshape(B, C, L * KS) + f64(bt)[None, :, None]
    y = (unpack4(w1_words, w1_scales).T @ mxq(up, 1, "e4m3")) + f64(b1)[None, :, None]
    y = np.tile(y, (1, 1, R))
    y = y.reshape(B, NL, 2 * BH, L * KS * R)
    return np.ascontiguousarray(y.transpose(2, 0, 1, 3))


def e4m3fn_bytes(y):
    return np.clip(np.asarray(y, np.float64), -448.0, 448.0).astype(np.float32).astype(ml_dtypes.float8_e4m3fn).view(np.uint8)


def e4m3fn_values(b):
    return np.asarray(b, np.uint8).view(ml_dtypes.float8_e4m3fn).astype(np.float64)


def setup_inputs():
    d = draw0()
    x0 = np.asarray(d['local_features']).astype(np.float64)
    s = (np.max(np.abs(x0), axis=(0, 1), keepdims=True) / 448.0).astype(np.float32)
    out = {}
    for k, v in d.items():
        if k == 'local_features':
            out['local_features_bytes'] = e4m3fn_bytes(x0 / s.astype(np.float64))
            out['local_features_scale'] = s
        else:
            out[k] = v
    return out


def reference(local_features_bytes, local_features_scale, wt, bt, w1_words, w1_scales, b1):
    return core(e4m3fn_values(local_features_bytes) * local_features_scale.astype(np.float64), wt, bt, w1_words, w1_scales, b1)

@@ -1,0 +1,265 @@
+from contextlib import ExitStack
+
+import concourse.mybir as mybir
+from concourse.masks import make_identity
+
+P = 128
+C = 512
+L = 128
+KS = 4
+T = 4
+NL = 24
+R = 4
+HALVES = 2
+LH = L // HALVES
+W = L * KS
+
+F32 = mybir.dt.float32
+BF16 = mybir.dt.bfloat16
+I32 = mybir.dt.int32
+U32 = mybir.dt.uint32
+U8 = mybir.dt.uint8
+FP8 = mybir.dt.float8_e4m3fn
+FP8X4 = mybir.dt.float8_e4m3fn_x4
+FP4X4 = mybir.dt.float4_e2m1fn_x4
+ADD = mybir.AluOpType.add
+MULT = mybir.AluOpType.mult
+IDENTITY = mybir.ActivationFunctionType.Identity
+
+FLOPS = 2 * (L * C * C * KS + NL * 128 * C * W)
+
+CHUNKS = ((0, 16, 2), (16, 16, 2), (32, 32, 2), (64, 32, 2), (96, 32, 2))
+WARM = (0, 0, 3, 3, 0)
+EARLY = 8
+AHEAD = 3
+SCALAR_TAP = 0
+
+
+def tile_conditionalfeaturesupsample_w4_kernel(
+    tc, features_bytes, features_scale, wt, bt, w1_words, w1_scales, b1, out
+):
+    nc = tc.nc
+    with ExitStack() as ctx:
+        keep = ctx.enter_context(tc.tile_pool(name="keep", bufs=1))
+        stage = ctx.enter_context(tc.tile_pool(name="stage", bufs=4))
+        psum = ctx.enter_context(tc.psum_pool(name="psum", bufs=6))
+        ctx.enter_context(tc.manual_schedule())
+
+        x_bytes = keep.tile([P, C], U8, align_bytes=64)
+        nc.sync.dma_start(out=x_bytes[:], in_=features_bytes.rearrange("b l c -> (b l) c"))
+        x_scale = keep.tile([P, T], F32)
+        nc.sync.dma_start(out=x_scale[:], in_=features_scale.rearrange("a b (p t) -> p (a b t)", t=T))
+
+        wt_rows = wt.rearrange("(p j) o k -> p j (o k)", j=T)
+        raw = []
+        for m0, count, vector_slots in CHUNKS:
+            raw_c = stage.tile([P, T, count * T * KS], BF16, align_bytes=64, bufs=len(CHUNKS))
+            nc.sync.dma_start(out=raw_c[:], in_=wt_rows[:, :, m0 * T * KS : (m0 + count) * T * KS])
+            raw.append(raw_c)
+
+        ident = keep.tile([P, P], BF16)
+        make_identity(nc, ident[:])
+        w1_parts = []
+        for n0, n1 in ((0, EARLY), (EARLY, NL)):
+            codes = keep.tile([P, 256 * (n1 - n0)], U8, align_bytes=64, tag=f"w1_codes_{n0}")
+            scales = keep.tile([P, 128 * (n1 - n0)], U8, align_bytes=64, tag=f"w1_scales_{n0}")
+            nc.gpsimd.memset(scales[:].bitcast(I32), 0)
+            w1_parts.append((n0, n1, codes, scales))
+        b1_rows = keep.tile([P, 128], BF16)
+        nc.vector.memset(b1_rows[:], 0.0)
+        table = keep.tile([P, 1], F32)
+        nc.scalar.activation(out=table[:], in_=b1_rows[:, 0:1], func=IDENTITY, bias=0.0)
+        bt_sb = keep.tile([P, T], BF16)
+        nc.scalar.dma_start(out=bt_sb[:], in_=bt.rearrange("(p t) -> p t", t=T))
+
+        scale_rows = w1_scales.rearrange("g q n -> (g q) n").bitcast(I32)
+        word_rows = w1_words.rearrange("g p n -> (g p) n").bitcast(I32)
+        for n0, n1, codes, scales in w1_parts:
+            for quad in range(4):
+                nc.sync.dma_start(
+                    out=scales[32 * quad : 32 * quad + 4, :].bitcast(I32),
+                    in_=scale_rows[4 * quad : 4 * quad + 4, 32 * n0 : 32 * n1],
+                )
+            nc.sync.dma_start(out=codes[:].bitcast(I32), in_=word_rows[:, 64 * n0 : 64 * n1])
+            if n0 == 0:
+                nc.sync.dma_start(out=b1_rows[0:NL, :], in_=b1.rearrange("(n j) -> n j", j=128))
+
+        x_wide = keep.tile([P, C], BF16, align_bytes=64)
+        nc.vector.tensor_copy(out=x_wide[:], in_=x_bytes[:].bitcast(FP8))
+        turned = psum.tile([P, T + 1, L], BF16, tag="turn", bufs=1)
+        for t in range(T):
+            nc.tensor.transpose(turned[:, t, :], x_wide[:, t::T], ident[:])
+
+        x_grouped = keep.tile([P, L, T], BF16, align_bytes=64)
+        x_codes = keep.tile([P, L], U32, align_bytes=64)
+        x_scales = keep.tile([P, L], U8, align_bytes=64)
+
+        grouped = keep.tile([P, KS * T * P * T], BF16, align_bytes=64)
+        grouped_v = grouped[:].rearrange("p (k t m j) -> p k t m j", k=KS, t=T, m=P)
+        w_codes = keep.tile([P, KS * T * P], U32, align_bytes=64)
+        w_scales = keep.tile([P, KS * T * P], U8, align_bytes=64)
+
+        warm = psum.tile([P, 512], F32, tag="warm", bufs=1)
+
+        def interleave(c):
+            m0, count, vector_slots = CHUNKS[c]
+            src = raw[c][:].rearrange("p j (m t k) -> p t m j k", t=T, k=KS)
+            dst = grouped_v[:, :, :, m0 : m0 + count, :].rearrange("p k t m j -> p t m j k")
+            for t in range(T):
+                if t < vector_slots:
+                    nc.vector.tensor_copy(out=dst[:, t], in_=src[:, t])
+                else:
+                    nc.scalar.copy(out=dst[:, t], in_=src[:, t])
+            for i in range(WARM[c]):
+                nc.tensor.matmul(warm[:], lhsT=ident[:], rhs=raw[c][:, i, :], start=True, stop=True)
+
+        def quantize_w(k, t, half):
+            c0 = (k * T + t) * P + half * 64
+            nc.vector.quantize_mx(
+                out=w_codes[:, c0 : c0 + 64].bitcast(FP8X4),
+                scales=w_scales[:, c0 : c0 + 64],
+                in_=grouped[:, T * c0 : T * (c0 + 64)],
+            )
+
+        interleave(0)
+        nc.vector.tensor_tensor(
+            out=x_grouped[:],
+            in0=turned[:, 0:T, :].rearrange("p t l -> p l t"),
+            in1=x_scale[:].unsqueeze(1).to_broadcast([P, L, T]),
+            op=MULT,
+        )
+        interleave(1)
+        nc.vector.quantize_mx(
+            out=x_codes[:].bitcast(FP8X4), scales=x_scales[:], in_=x_grouped[:].rearrange("p l t -> p (l t)")
+        )
+        interleave(2)
+        for t in range(T):
+            for k in range(KS):
+                quantize_w(k, t, 0)
+        interleave(3)
+        interleave(4)
+
+        up_grouped = keep.tile([P, HALVES, KS, LH, T], BF16, align_bytes=64)
+        up_codes = keep.tile([P, HALVES * KS * LH], U32, align_bytes=64)
+        up_scales = keep.tile([P, HALVES * KS * LH], U8, align_bytes=64)
+        up_acc = []
+
+        for k in range(KS):
+            acc_k = psum.tile([P, T, L], F32, tag="acc", bufs=6)
+            up_acc.append(acc_k)
+
+        def finish_w(k, t):
+            quantize_w(k, t, 1)
+            c0 = (k * T + t) * P
+            nc.tensor.matmul_mx(
+                out=up_acc[k][:, t, :],
+                lhsT=w_codes[:, c0 : c0 + P].bitcast(FP8X4),
+                lhsT_scale=w_scales[:, c0 : c0 + P],
+                rhs=x_codes[:].bitcast(FP8X4),
+                rhs_scale=x_scales[:],
+                start=True,
+                stop=True,
+            )
+
+        def add_bias(k, half):
+            src = up_acc[k][:, :, half * LH : (half + 1) * LH]
+            if k == SCALAR_TAP:
+                for t in range(T):
+                    nc.scalar.activation(
+                        out=up_grouped[:, half, k, :, t], in_=src[:, t, :], func=IDENTITY, bias=bt_sb[:, t : t + 1]
+                    )
+            else:
+                nc.vector.tensor_tensor(
+                    out=up_grouped[:, half, k],
+                    in0=src.rearrange("p t l -> p l t"),
+                    in1=bt_sb[:].unsqueeze(1).to_broadcast([P, LH, T]),
+                    op=ADD,
+                )
+
+        def quantize_up(half):
+            cols = slice(half * KS * LH, (half + 1) * KS * LH)
+            nc.vector.quantize_mx(
+                out=up_codes[:, cols].bitcast(FP8X4),
+                scales=up_scales[:, cols],
+                in_=up_grouped[:, half].rearrange("p k l t -> p (k l t)"),
+            )
+
+        own = CHUNKS[-1][2]
+        for k in range(AHEAD):
+            for t in range(own):
+                finish_w(k, t)
+        for k in range(KS):
+            for t in range(own if k < AHEAD else 0, T):
+                finish_w(k, t)
+        for half in range(HALVES):
+            add_bias(SCALAR_TAP, half)
+        nc.tensor.transpose(turned[:, T, :], b1_rows[:], ident[:])
+        b1_cols = keep.tile([P, NL], F32)
+        nc.scalar.copy(out=b1_cols[:], in_=turned[:, T, 0:NL])
+        add_bias(1, 0)
+        add_bias(2, 0)
+        add_bias(3, 0)
+        add_bias(1, 1)
+        quantize_up(0)
+        add_bias(2, 1)
+        add_bias(3, 1)
+
+        out_rows = out.rearrange("j b n (r w) -> j (b n) r w", r=R)
+
+        def multiply_w1(n, dst, cols):
+            n0, _, codes, scales = w1_parts[0] if n < EARLY else w1_parts[1]
+            nc.tensor.matmul_mx(
+                out=dst,
+                lhsT=codes[:, 256 * (n - n0) : 256 * (n - n0 + 1)].bitcast(FP4X4),
+                lhsT_scale=scales[:, 128 * (n - n0) : 128 * (n - n0 + 1)],
+                rhs=up_codes[:, cols].bitcast(FP8X4),
+                rhs_scale=up_scales[:, cols],
+                start=True,
+                stop=True,
+            )
+
+        def empty(n, dst, src):
+            if n % 2 == 0:
+                nc.scalar.activation(out=dst, in_=src, func=IDENTITY, bias=b1_cols[:, n : n + 1])
+            else:
+                nc.vector.tensor_scalar(out=dst, in0=src, scalar1=b1_cols[:, n : n + 1], scalar2=None, op0=ADD)
+
+        for half in range(HALVES):
+            if half == 1:
+                quantize_up(1)
+            acc_half = psum.tile([P, KS, LH], F32, tag="acc", bufs=6)
+            multiply_w1(0, acc_half[:].rearrange("p k l -> p (k l)"), slice(half * KS * LH, (half + 1) * KS * LH))
+            y_half = stage.tile([P, LH * KS], F32, tag="y_half", bufs=2)
+            empty(0, y_half[:].rearrange("p (l k) -> p l k", k=KS), acc_half[:].rearrange("p k l -> p l k"))
+            nc.sync.dma_start(
+                out=out_rows[:, 0, :, half * LH * KS : (half + 1) * LH * KS],
+                in_=y_half[:].unsqueeze(1).to_broadcast([P, R, LH * KS]),
+            )
+
+        def layer(n):
+            acc = psum.tile([P, HALVES, KS, LH], F32, tag="acc", bufs=6)
+            multiply_w1(n, acc[:].rearrange("p h k l -> p (h k l)"), slice(0, W))
+            return acc
+
+        acc_1 = layer(1)
+        y_once = stage.tile([P, W], F32, tag="y_once", bufs=1)
+        empty(
+            1,
+            y_once[:].rearrange("p (h l k) -> p h l k", h=HALVES, k=KS),
+            acc_1[:].rearrange("p h k l -> p h l k"),
+        )
+        nc.sync.dma_start(out=out_rows[:, 1], in_=y_once[:].unsqueeze(1).to_broadcast([P, R, W]))
+
+        n = 2
+        for size in (1, 1, 2, 4, 4, 4, 4, 2):
+            y_group = stage.tile([P, 4, R, W], F32, tag="y_group", bufs=4)
+            for i in range(size):
+                acc_n = layer(n + i)
+                for half in range(HALVES):
+                    empty(
+                        n + i,
+                        y_group[:, i, :, half * LH * KS : (half + 1) * LH * KS].rearrange("p r (l k) -> p r l k", k=KS),
+                        acc_n[:, half].rearrange("p k l -> p l k").unsqueeze(1).to_broadcast([P, R, LH, KS]),
+                    )
+            nc.sync.dma_start(out=out_rows[:, n : n + size], in_=y_group[:, 0:size])
+            n += size

@@ -10,8 +10,9 @@ KS = 4
 T = 4
 NL = 24
 R = 4
-HALVES = 2
-LH = L // HALVES
+Q = 4
+LQ = L // Q
+WQ = LQ * KS
 W = L * KS
 
 F32 = mybir.dt.float32
@@ -28,11 +29,10 @@ IDENTITY = mybir.ActivationFunctionType.Identity
 
 FLOPS = 2 * (L * C * C * KS + NL * 128 * C * W)
 
-CHUNKS = ((0, 16, 2), (16, 16, 2), (32, 32, 2), (64, 32, 2), (96, 32, 2))
-WARM = (0, 0, 3, 3, 0)
-EARLY = 8
-AHEAD = 3
-SCALAR_TAP = 0
+CHUNKS = ((16, 2), (16, 2), (32, 2), (32, 2), (32, 2))
+WARM = (0, 0, 2, 2, 0)
+FIRST_PARTS = (1, 1, 2, 2)
+GROUPS = (4, 8, 8)
 
 
 def tile_conditionalfeaturesupsample_w4_kernel(
@@ -41,8 +41,7 @@ def tile_conditionalfeaturesupsample_w4_kernel(
     nc = tc.nc
     with ExitStack() as ctx:
         keep = ctx.enter_context(tc.tile_pool(name="keep", bufs=1))
-        stage = ctx.enter_context(tc.tile_pool(name="stage", bufs=4))
-        psum = ctx.enter_context(tc.psum_pool(name="psum", bufs=6))
+        psum = ctx.enter_context(tc.psum_pool(name="psum", bufs=7))
         ctx.enter_context(tc.manual_schedule())
 
         x_bytes = keep.tile([P, C], U8, align_bytes=64)
@@ -52,41 +51,36 @@ def tile_conditionalfeaturesupsample_w4_kernel(
 
         wt_rows = wt.rearrange("(p j) o k -> p j (o k)", j=T)
         raw = []
-        for m0, count, vector_slots in CHUNKS:
-            raw_c = stage.tile([P, T, count * T * KS], BF16, align_bytes=64, bufs=len(CHUNKS))
+        starts = []
+        m0 = 0
+        for c, (count, vector_slots) in enumerate(CHUNKS):
+            raw_c = keep.tile([P, T, count * T * KS], BF16, align_bytes=64, tag=f"raw_{c}")
             nc.sync.dma_start(out=raw_c[:], in_=wt_rows[:, :, m0 * T * KS : (m0 + count) * T * KS])
             raw.append(raw_c)
+            starts.append(m0)
+            m0 += count
+        bt_sb = keep.tile([P, T], BF16)
+        nc.sync.dma_start(out=bt_sb[:], in_=bt.rearrange("(p t) -> p t", t=T))
 
         ident = keep.tile([P, P], BF16)
         make_identity(nc, ident[:])
-        w1_parts = []
-        for n0, n1 in ((0, EARLY), (EARLY, NL)):
-            codes = keep.tile([P, 256 * (n1 - n0)], U8, align_bytes=64, tag=f"w1_codes_{n0}")
-            scales = keep.tile([P, 128 * (n1 - n0)], U8, align_bytes=64, tag=f"w1_scales_{n0}")
-            nc.gpsimd.memset(scales[:].bitcast(I32), 0)
-            w1_parts.append((n0, n1, codes, scales))
+        w1_codes = keep.tile([P, 256 * NL], U8, align_bytes=64)
+        w1_plane = keep.tile([P, 128 * NL], U8, align_bytes=64)
+        nc.vector.memset(w1_plane[:].bitcast(I32), 0)
         b1_rows = keep.tile([P, 128], BF16)
-        nc.vector.memset(b1_rows[:], 0.0)
-        table = keep.tile([P, 1], F32)
-        nc.scalar.activation(out=table[:], in_=b1_rows[:, 0:1], func=IDENTITY, bias=0.0)
-        bt_sb = keep.tile([P, T], BF16)
-        nc.scalar.dma_start(out=bt_sb[:], in_=bt.rearrange("(p t) -> p t", t=T))
+        nc.scalar.activation(out=b1_rows[:], in_=ident[:], func=IDENTITY, scale=0.0)
+        nc.sync.dma_start(out=b1_rows[0:NL, :], in_=b1.rearrange("(n j) -> n j", j=128))
 
         scale_rows = w1_scales.rearrange("g q n -> (g q) n").bitcast(I32)
-        word_rows = w1_words.rearrange("g p n -> (g p) n").bitcast(I32)
-        for n0, n1, codes, scales in w1_parts:
-            for quad in range(4):
-                nc.sync.dma_start(
-                    out=scales[32 * quad : 32 * quad + 4, :].bitcast(I32),
-                    in_=scale_rows[4 * quad : 4 * quad + 4, 32 * n0 : 32 * n1],
-                )
-            nc.sync.dma_start(out=codes[:].bitcast(I32), in_=word_rows[:, 64 * n0 : 64 * n1])
-            if n0 == 0:
-                nc.sync.dma_start(out=b1_rows[0:NL, :], in_=b1.rearrange("(n j) -> n j", j=128))
+        for quad in range(4):
+            nc.sync.dma_start(
+                out=w1_plane[32 * quad : 32 * quad + 4, :].bitcast(I32), in_=scale_rows[4 * quad : 4 * quad + 4, :]
+            )
+        nc.sync.dma_start(out=w1_codes[:].bitcast(I32), in_=w1_words.rearrange("g p n -> (g p) n").bitcast(I32))
 
         x_wide = keep.tile([P, C], BF16, align_bytes=64)
         nc.vector.tensor_copy(out=x_wide[:], in_=x_bytes[:].bitcast(FP8))
-        turned = psum.tile([P, T + 1, L], BF16, tag="turn", bufs=1)
+        turned = psum.tile([P, T, L], BF16, tag="turn", bufs=1)
         for t in range(T):
             nc.tensor.transpose(turned[:, t, :], x_wide[:, t::T], ident[:])
 
@@ -99,19 +93,19 @@ def tile_conditionalfeaturesupsample_w4_kernel(
         w_codes = keep.tile([P, KS * T * P], U32, align_bytes=64)
         w_scales = keep.tile([P, KS * T * P], U8, align_bytes=64)
 
-        warm = psum.tile([P, 512], F32, tag="warm", bufs=1)
+        warm = psum.tile([P, 512], F32, tag="acc")
 
         def interleave(c):
-            m0, count, vector_slots = CHUNKS[c]
+            count, vector_slots = CHUNKS[c]
             src = raw[c][:].rearrange("p j (m t k) -> p t m j k", t=T, k=KS)
-            dst = grouped_v[:, :, :, m0 : m0 + count, :].rearrange("p k t m j -> p t m j k")
+            dst = grouped_v[:, :, :, starts[c] : starts[c] + count, :].rearrange("p k t m j -> p t m j k")
             for t in range(T):
                 if t < vector_slots:
                     nc.vector.tensor_copy(out=dst[:, t], in_=src[:, t])
                 else:
                     nc.scalar.copy(out=dst[:, t], in_=src[:, t])
             for i in range(WARM[c]):
-                nc.tensor.matmul(warm[:], lhsT=ident[:], rhs=raw[c][:, i, :], start=True, stop=True)
+                nc.tensor.matmul(warm[:], lhsT=ident[:], rhs=raw[c][:, i, 0:512], start=True, stop=True)
 
         def quantize_w(k, t, half):
             c0 = (k * T + t) * P + half * 64
@@ -121,31 +115,36 @@ def tile_conditionalfeaturesupsample_w4_kernel(
                 in_=grouped[:, T * c0 : T * (c0 + 64)],
             )
 
-        interleave(0)
+        first_half = [c for c in range(len(CHUNKS)) if starts[c] < 64]
+        second_half = [c for c in range(len(CHUNKS)) if starts[c] >= 64]
+        for c in first_half[:2]:
+            interleave(c)
         nc.vector.tensor_tensor(
             out=x_grouped[:],
-            in0=turned[:, 0:T, :].rearrange("p t l -> p l t"),
+            in0=turned[:].rearrange("p t l -> p l t"),
             in1=x_scale[:].unsqueeze(1).to_broadcast([P, L, T]),
             op=MULT,
         )
-        interleave(1)
         nc.vector.quantize_mx(
             out=x_codes[:].bitcast(FP8X4), scales=x_scales[:], in_=x_grouped[:].rearrange("p l t -> p (l t)")
         )
-        interleave(2)
+        for c in first_half[2:]:
+            interleave(c)
         for t in range(T):
             for k in range(KS):
                 quantize_w(k, t, 0)
-        interleave(3)
-        interleave(4)
+        for c in second_half:
+            interleave(c)
 
-        up_grouped = keep.tile([P, HALVES, KS, LH, T], BF16, align_bytes=64)
-        up_codes = keep.tile([P, HALVES * KS * LH], U32, align_bytes=64)
-        up_scales = keep.tile([P, HALVES * KS * LH], U8, align_bytes=64)
+        b1_turned = psum.tile([P, NL], F32, tag="turn", bufs=1)
+        nc.tensor.matmul(b1_turned[:], lhsT=b1_rows[:], rhs=ident[:, 0:NL], start=True, stop=True)
+
+        up_grouped = keep.tile([P, Q, KS, LQ, T], BF16, align_bytes=64)
+        up_codes = keep.tile([P, W], U32, align_bytes=64)
+        up_scales = keep.tile([P, W], U8, align_bytes=64)
         up_acc = []
-
         for k in range(KS):
-            acc_k = psum.tile([P, T, L], F32, tag="acc", bufs=6)
+            acc_k = psum.tile([P, T, L], F32, tag="acc")
             up_acc.append(acc_k)
 
         def finish_w(k, t):
@@ -161,105 +160,100 @@ def tile_conditionalfeaturesupsample_w4_kernel(
                 stop=True,
             )
 
-        def add_bias(k, half):
-            src = up_acc[k][:, :, half * LH : (half + 1) * LH]
-            if k == SCALAR_TAP:
-                for t in range(T):
-                    nc.scalar.activation(
-                        out=up_grouped[:, half, k, :, t], in_=src[:, t, :], func=IDENTITY, bias=bt_sb[:, t : t + 1]
-                    )
-            else:
-                nc.vector.tensor_tensor(
-                    out=up_grouped[:, half, k],
-                    in0=src.rearrange("p t l -> p l t"),
-                    in1=bt_sb[:].unsqueeze(1).to_broadcast([P, LH, T]),
-                    op=ADD,
+        def add_bias(k, q0, q1):
+            src = up_acc[k][:, :, q0 * LQ : q1 * LQ].rearrange("p t (q l) -> p q l t", l=LQ)
+            nc.vector.tensor_tensor(
+                out=up_grouped[:, q0:q1, k],
+                in0=src,
+                in1=bt_sb[:].unsqueeze(1).unsqueeze(1).to_broadcast([P, q1 - q0, LQ, T]),
+                op=ADD,
+            )
+
+        def add_bias_scalar(k, q0, q1):
+            src = up_acc[k][:, :, q0 * LQ : q1 * LQ].rearrange("p t (q l) -> p q l t", l=LQ)
+            for t in range(T):
+                nc.scalar.activation(
+                    out=up_grouped[:, q0:q1, k, :, t], in_=src[:, :, :, t], func=IDENTITY, bias=bt_sb[:, t : t + 1]
                 )
 
-        def quantize_up(half):
-            cols = slice(half * KS * LH, (half + 1) * KS * LH)
+        def quantize_up(q0, q1):
             nc.vector.quantize_mx(
-                out=up_codes[:, cols].bitcast(FP8X4),
-                scales=up_scales[:, cols],
-                in_=up_grouped[:, half].rearrange("p k l t -> p (k l t)"),
+                out=up_codes[:, q0 * WQ : q1 * WQ].bitcast(FP8X4),
+                scales=up_scales[:, q0 * WQ : q1 * WQ],
+                in_=up_grouped[:, q0:q1].rearrange("p q k l t -> p (q k l t)"),
             )
 
-        own = CHUNKS[-1][2]
-        for k in range(AHEAD):
-            for t in range(own):
+        own = CHUNKS[-1][1]
+        for t in range(own):
+            for k in range(KS):
                 finish_w(k, t)
         for k in range(KS):
-            for t in range(own if k < AHEAD else 0, T):
+            for t in range(own, T):
                 finish_w(k, t)
-        for half in range(HALVES):
-            add_bias(SCALAR_TAP, half)
-        nc.tensor.transpose(turned[:, T, :], b1_rows[:], ident[:])
-        b1_cols = keep.tile([P, NL], F32)
-        nc.scalar.copy(out=b1_cols[:], in_=turned[:, T, 0:NL])
-        add_bias(1, 0)
-        add_bias(2, 0)
-        add_bias(3, 0)
-        add_bias(1, 1)
-        quantize_up(0)
-        add_bias(2, 1)
-        add_bias(3, 1)
 
         out_rows = out.rearrange("j b n (r w) -> j (b n) r w", r=R)
+        b1_cols = keep.tile([P, NL], F32)
 
-        def multiply_w1(n, dst, cols):
-            n0, _, codes, scales = w1_parts[0] if n < EARLY else w1_parts[1]
-            nc.tensor.matmul_mx(
-                out=dst,
-                lhsT=codes[:, 256 * (n - n0) : 256 * (n - n0 + 1)].bitcast(FP4X4),
-                lhsT_scale=scales[:, 128 * (n - n0) : 128 * (n - n0 + 1)],
-                rhs=up_codes[:, cols].bitcast(FP8X4),
-                rhs_scale=up_scales[:, cols],
-                start=True,
-                stop=True,
+        def layer(n, q0, q1, dst):
+            acc = psum.tile([P, q1 - q0, KS, LQ], F32, tag="acc")
+            flat = acc[:].rearrange("p q k l -> p (q k l)")
+            spans = ((q0, q0 + 1), (q0 + 1, q1)) if q1 - q0 == 3 else ((q0, q1),)
+            for a, b in spans:
+                nc.tensor.matmul_mx(
+                    out=flat[:, (a - q0) * WQ : (b - q0) * WQ],
+                    lhsT=w1_codes[:, 256 * n : 256 * (n + 1)].bitcast(FP4X4),
+                    lhsT_scale=w1_plane[:, 128 * n : 128 * (n + 1)],
+                    rhs=up_codes[:, a * WQ : b * WQ].bitcast(FP8X4),
+                    rhs_scale=up_scales[:, a * WQ : b * WQ],
+                    start=True,
+                    stop=True,
+                )
+            nc.scalar.activation(
+                out=dst.rearrange("p (q l k) -> p q l k", l=LQ, k=KS),
+                in_=acc[:].rearrange("p q k l -> p q l k"),
+                func=IDENTITY,
+                bias=b1_cols[:, n : n + 1],
             )
 
-        def empty(n, dst, src):
-            if n % 2 == 0:
-                nc.scalar.activation(out=dst, in_=src, func=IDENTITY, bias=b1_cols[:, n : n + 1])
-            else:
-                nc.vector.tensor_scalar(out=dst, in0=src, scalar1=b1_cols[:, n : n + 1], scalar2=None, op0=ADD)
-
-        for half in range(HALVES):
-            if half == 1:
-                quantize_up(1)
-            acc_half = psum.tile([P, KS, LH], F32, tag="acc", bufs=6)
-            multiply_w1(0, acc_half[:].rearrange("p k l -> p (k l)"), slice(half * KS * LH, (half + 1) * KS * LH))
-            y_half = stage.tile([P, LH * KS], F32, tag="y_half", bufs=2)
-            empty(0, y_half[:].rearrange("p (l k) -> p l k", k=KS), acc_half[:].rearrange("p k l -> p l k"))
+        def part(n, q0, q1):
+            y_part = keep.tile([P, (q1 - q0) * WQ], F32, tag=f"y_{n}_{q0}")
+            layer(n, q0, q1, y_part[:])
             nc.sync.dma_start(
-                out=out_rows[:, 0, :, half * LH * KS : (half + 1) * LH * KS],
-                in_=y_half[:].unsqueeze(1).to_broadcast([P, R, LH * KS]),
+                out=out_rows[:, n, :, q0 * WQ : q1 * WQ],
+                in_=y_part[:].unsqueeze(1).to_broadcast([P, R, (q1 - q0) * WQ]),
             )
 
-        def layer(n):
-            acc = psum.tile([P, HALVES, KS, LH], F32, tag="acc", bufs=6)
-            multiply_w1(n, acc[:].rearrange("p h k l -> p (h k l)"), slice(0, W))
-            return acc
+        nc.scalar.copy(out=b1_cols[:], in_=b1_turned[:])
+        add_bias(0, 0, 2)
+        add_bias_scalar(0, 2, Q)
+        for k in range(1, KS):
+            add_bias(k, 0, 1)
+        add_bias(1, 1, 2)
+        quantize_up(0, 1)
+        for n, quarters in enumerate(FIRST_PARTS):
+            if quarters == 1:
+                part(n, 0, 1)
+        add_bias(2, 1, 2)
+        add_bias(3, 1, 2)
+        add_bias(1, 2, Q)
+        quantize_up(1, 2)
+        for n, quarters in enumerate(FIRST_PARTS):
+            if quarters == 2:
+                part(n, 0, 2)
+        add_bias(2, 2, Q)
+        add_bias(3, 2, Q)
+        quantize_up(2, Q)
+        for n, quarters in enumerate(FIRST_PARTS):
+            part(n, quarters, Q)
 
-        acc_1 = layer(1)
-        y_once = stage.tile([P, W], F32, tag="y_once", bufs=1)
-        empty(
-            1,
-            y_once[:].rearrange("p (h l k) -> p h l k", h=HALVES, k=KS),
-            acc_1[:].rearrange("p h k l -> p h l k"),
-        )
-        nc.sync.dma_start(out=out_rows[:, 1], in_=y_once[:].unsqueeze(1).to_broadcast([P, R, W]))
-
-        n = 2
-        for size in (1, 1, 2, 4, 4, 4, 4, 2):
-            y_group = stage.tile([P, 4, R, W], F32, tag="y_group", bufs=4)
+        n = len(FIRST_PARTS)
+        for size in GROUPS:
+            y_group = keep.tile([P, size, R, W], F32, tag=f"y_group_{n}")
             for i in range(size):
-                acc_n = layer(n + i)
-                for half in range(HALVES):
-                    empty(
-                        n + i,
-                        y_group[:, i, :, half * LH * KS : (half + 1) * LH * KS].rearrange("p r (l k) -> p r l k", k=KS),
-                        acc_n[:, half].rearrange("p k l -> p l k").unsqueeze(1).to_broadcast([P, R, LH, KS]),
-                    )
-            nc.sync.dma_start(out=out_rows[:, n : n + size], in_=y_group[:, 0:size])
+                layer(n + i, 0, Q, y_group[:, i, 0, :])
+                nc.vector.tensor_copy(
+                    out=y_group[:, i, 1:R, :].rearrange("p r (h w) -> p h r w", h=2),
+                    in_=y_group[:, i, 0, :].rearrange("p (h w) -> p h w", h=2).unsqueeze(2).to_broadcast([P, 2, R - 1, W // 2]),
+                )
+            nc.sync.dma_start(out=out_rows[:, n : n + size], in_=y_group[:])
             n += size

@@ -30,7 +30,7 @@ IDENTITY = mybir.ActivationFunctionType.Identity
 FLOPS = 2 * (L * C * C * KS + NL * 128 * C * W)
 
 CHUNKS = ((16, 2), (16, 2), (32, 2), (32, 2), (32, 2))
-WARM = (0, 0, 2, 2, 0)
+WARM = (0, 0, 1, 1, 1)
 FIRST_PARTS = (1, 1, 2, 2)
 GROUPS = (4, 8, 8)
 
@@ -93,7 +93,7 @@ def tile_conditionalfeaturesupsample_w4_kernel(
         w_codes = keep.tile([P, KS * T * P], U32, align_bytes=64)
         w_scales = keep.tile([P, KS * T * P], U8, align_bytes=64)
 
-        warm = psum.tile([P, 512], F32, tag="acc")
+        warm = psum.tile([P, 256], F32, tag="acc")
 
         def interleave(c):
             count, vector_slots = CHUNKS[c]
@@ -105,7 +105,8 @@ def tile_conditionalfeaturesupsample_w4_kernel(
                 else:
                     nc.scalar.copy(out=dst[:, t], in_=src[:, t])
             for i in range(WARM[c]):
-                nc.tensor.matmul(warm[:], lhsT=ident[:], rhs=raw[c][:, i, 0:512], start=True, stop=True)
+                words = raw[c][:].rearrange("p j n -> p (j n)").bitcast(F32)
+                nc.tensor.matmul(warm[:], lhsT=words[:, 0:P], rhs=words[:, 0:256], start=True, stop=True)
 
         def quantize_w(k, t, half):
             c0 = (k * T + t) * P + half * 64

@@ -31,8 +31,8 @@ FLOPS = 2 * (L * C * C * KS + NL * 128 * C * W)
 
 CHUNKS = ((16, 2), (16, 2), (32, 2), (32, 2), (32, 2))
 WARM = (0, 0, 1, 1, 1)
-FIRST_PARTS = (1, 1, 2, 2)
-GROUPS = (4, 8, 8)
+FIRST_PARTS = (2, 2)
+GROUPS = (2, 6, 7, 7)
 
 
 def tile_conditionalfeaturesupsample_w4_kernel(
@@ -228,19 +228,12 @@ def tile_conditionalfeaturesupsample_w4_kernel(
         add_bias(0, 0, 2)
         add_bias_scalar(0, 2, Q)
         for k in range(1, KS):
-            add_bias(k, 0, 1)
-        add_bias(1, 1, 2)
-        quantize_up(0, 1)
-        for n, quarters in enumerate(FIRST_PARTS):
-            if quarters == 1:
-                part(n, 0, 1)
-        add_bias(2, 1, 2)
-        add_bias(3, 1, 2)
+            add_bias(k, 0, 2)
         add_bias(1, 2, Q)
-        quantize_up(1, 2)
+        quantize_up(0, 2)
         for n, quarters in enumerate(FIRST_PARTS):
-            if quarters == 2:
-                part(n, 0, 2)
+            if quarters:
+                part(n, 0, quarters)
         add_bias(2, 2, Q)
         add_bias(3, 2, Q)
         quantize_up(2, Q)
@@ -249,7 +242,7 @@ def tile_conditionalfeaturesupsample_w4_kernel(
 
         n = len(FIRST_PARTS)
         for size in GROUPS:
-            y_group = keep.tile([P, size, R, W], F32, tag=f"y_group_{n}")
+            y_group = keep.tile([P, size, R, W], F32, tag="y_group", bufs=3)
             for i in range(size):
                 layer(n + i, 0, Q, y_group[:, i, 0, :])
                 nc.vector.tensor_copy(

@@ -10,9 +10,9 @@ KS = 4
 T = 4
 NL = 24
 R = 4
-Q = 4
-LQ = L // Q
-WQ = LQ * KS
+HALVES = 2
+LH = L // HALVES
+WH = LH * KS
 W = L * KS
 
 F32 = mybir.dt.float32
@@ -31,7 +31,6 @@ FLOPS = 2 * (L * C * C * KS + NL * 128 * C * W)
 
 CHUNKS = ((16, 2), (16, 2), (32, 2), (32, 2), (32, 2))
 WARM = (0, 0, 1, 1, 1)
-FIRST_PARTS = (2, 2)
 GROUPS = (2, 6, 7, 7)
 
 
@@ -140,7 +139,7 @@ def tile_conditionalfeaturesupsample_w4_kernel(
         b1_turned = psum.tile([P, NL], F32, tag="turn", bufs=1)
         nc.tensor.matmul(b1_turned[:], lhsT=b1_rows[:], rhs=ident[:, 0:NL], start=True, stop=True)
 
-        up_grouped = keep.tile([P, Q, KS, LQ, T], BF16, align_bytes=64)
+        up_grouped = keep.tile([P, HALVES, KS, LH, T], BF16, align_bytes=64)
         up_codes = keep.tile([P, W], U32, align_bytes=64)
         up_scales = keep.tile([P, W], U8, align_bytes=64)
         up_acc = []
@@ -161,27 +160,28 @@ def tile_conditionalfeaturesupsample_w4_kernel(
                 stop=True,
             )
 
-        def add_bias(k, q0, q1):
-            src = up_acc[k][:, :, q0 * LQ : q1 * LQ].rearrange("p t (q l) -> p q l t", l=LQ)
+        def add_bias(k, half):
             nc.vector.tensor_tensor(
-                out=up_grouped[:, q0:q1, k],
-                in0=src,
-                in1=bt_sb[:].unsqueeze(1).unsqueeze(1).to_broadcast([P, q1 - q0, LQ, T]),
+                out=up_grouped[:, half, k],
+                in0=up_acc[k][:, :, half * LH : (half + 1) * LH].rearrange("p t l -> p l t"),
+                in1=bt_sb[:].unsqueeze(1).to_broadcast([P, LH, T]),
                 op=ADD,
             )
 
-        def add_bias_scalar(k, q0, q1):
-            src = up_acc[k][:, :, q0 * LQ : q1 * LQ].rearrange("p t (q l) -> p q l t", l=LQ)
+        def add_bias_scalar(k, half):
             for t in range(T):
                 nc.scalar.activation(
-                    out=up_grouped[:, q0:q1, k, :, t], in_=src[:, :, :, t], func=IDENTITY, bias=bt_sb[:, t : t + 1]
+                    out=up_grouped[:, half, k, :, t],
+                    in_=up_acc[k][:, t, half * LH : (half + 1) * LH],
+                    func=IDENTITY,
+                    bias=bt_sb[:, t : t + 1],
                 )
 
-        def quantize_up(q0, q1):
+        def quantize_up(half):
             nc.vector.quantize_mx(
-                out=up_codes[:, q0 * WQ : q1 * WQ].bitcast(FP8X4),
-                scales=up_scales[:, q0 * WQ : q1 * WQ],
-                in_=up_grouped[:, q0:q1].rearrange("p q k l t -> p (q k l t)"),
+                out=up_codes[:, half * WH : (half + 1) * WH].bitcast(FP8X4),
+                scales=up_scales[:, half * WH : (half + 1) * WH],
+                in_=up_grouped[:, half].rearrange("p k l t -> p (k l t)"),
             )
 
         own = CHUNKS[-1][1]
@@ -195,59 +195,63 @@ def tile_conditionalfeaturesupsample_w4_kernel(
         out_rows = out.rearrange("j b n (r w) -> j (b n) r w", r=R)
         b1_cols = keep.tile([P, NL], F32)
 
-        def layer(n, q0, q1, dst):
-            acc = psum.tile([P, q1 - q0, KS, LQ], F32, tag="acc")
-            flat = acc[:].rearrange("p q k l -> p (q k l)")
-            spans = ((q0, q0 + 1), (q0 + 1, q1)) if q1 - q0 == 3 else ((q0, q1),)
-            for a, b in spans:
-                nc.tensor.matmul_mx(
-                    out=flat[:, (a - q0) * WQ : (b - q0) * WQ],
-                    lhsT=w1_codes[:, 256 * n : 256 * (n + 1)].bitcast(FP4X4),
-                    lhsT_scale=w1_plane[:, 128 * n : 128 * (n + 1)],
-                    rhs=up_codes[:, a * WQ : b * WQ].bitcast(FP8X4),
-                    rhs_scale=up_scales[:, a * WQ : b * WQ],
-                    start=True,
-                    stop=True,
-                )
-            nc.scalar.activation(
-                out=dst.rearrange("p (q l k) -> p q l k", l=LQ, k=KS),
-                in_=acc[:].rearrange("p q k l -> p q l k"),
-                func=IDENTITY,
-                bias=b1_cols[:, n : n + 1],
+        def multiply(n, h0, h1):
+            acc = psum.tile([P, h1 - h0, KS, LH], F32, tag="acc")
+            nc.tensor.matmul_mx(
+                out=acc[:].rearrange("p h k l -> p (h k l)"),
+                lhsT=w1_codes[:, 256 * n : 256 * (n + 1)].bitcast(FP4X4),
+                lhsT_scale=w1_plane[:, 128 * n : 128 * (n + 1)],
+                rhs=up_codes[:, h0 * WH : h1 * WH].bitcast(FP8X4),
+                rhs_scale=up_scales[:, h0 * WH : h1 * WH],
+                start=True,
+                stop=True,
+            )
+            return acc[:].rearrange("p h k l -> p h l k")
+
+        def empty_scalar(n, dst, src):
+            nc.scalar.activation(out=dst, in_=src, func=IDENTITY, bias=b1_cols[:, n : n + 1])
+
+        def empty_vector(n, dst, src):
+            nc.vector.tensor_scalar(out=dst, in0=src, scalar1=b1_cols[:, n : n + 1], scalar2=None, op0=ADD)
+
+        def first_layer(half):
+            y_half = keep.tile([P, WH], F32, tag=f"y_half_{half}")
+            empty_scalar(0, y_half[:].rearrange("p (l k) -> p l k", k=KS), multiply(0, half, half + 1)[:, 0])
+            nc.sync.dma_start(
+                out=out_rows[:, 0, :, half * WH : (half + 1) * WH],
+                in_=y_half[:].unsqueeze(1).to_broadcast([P, R, WH]),
             )
 
-        def part(n, q0, q1):
-            y_part = keep.tile([P, (q1 - q0) * WQ], F32, tag=f"y_{n}_{q0}")
-            layer(n, q0, q1, y_part[:])
-            nc.sync.dma_start(
-                out=out_rows[:, n, :, q0 * WQ : q1 * WQ],
-                in_=y_part[:].unsqueeze(1).to_broadcast([P, R, (q1 - q0) * WQ]),
-            )
+        y_second = keep.tile([P, R, HALVES, LH, KS], F32)
+
+        def second_layer(half, empty):
+            empty(1, y_second[:, :, half], multiply(1, half, half + 1)[:, 0].unsqueeze(1).to_broadcast([P, R, LH, KS]))
 
         nc.scalar.copy(out=b1_cols[:], in_=b1_turned[:])
-        add_bias(0, 0, 2)
-        add_bias_scalar(0, 2, Q)
+        add_bias(0, 0)
+        add_bias_scalar(0, 1)
         for k in range(1, KS):
-            add_bias(k, 0, 2)
-        add_bias(1, 2, Q)
-        quantize_up(0, 2)
-        for n, quarters in enumerate(FIRST_PARTS):
-            if quarters:
-                part(n, 0, quarters)
-        add_bias(2, 2, Q)
-        add_bias(3, 2, Q)
-        quantize_up(2, Q)
-        for n, quarters in enumerate(FIRST_PARTS):
-            part(n, quarters, Q)
+            add_bias(k, 0)
+        add_bias(1, 1)
+        quantize_up(0)
+        first_layer(0)
+        second_layer(0, empty_scalar)
+        add_bias(2, 1)
+        add_bias(3, 1)
+        quantize_up(1)
+        first_layer(1)
+        second_layer(1, empty_vector)
+        nc.sync.dma_start(out=out_rows[:, 1], in_=y_second[:].rearrange("p r h l k -> p r (h l k)"))
 
-        n = len(FIRST_PARTS)
+        n = 2
         for size in GROUPS:
             y_group = keep.tile([P, size, R, W], F32, tag="y_group", bufs=3)
             for i in range(size):
-                layer(n + i, 0, Q, y_group[:, i, 0, :])
+                first_copy = y_group[:, i, 0, :]
+                empty_scalar(n + i, first_copy.rearrange("p (h l k) -> p h l k", h=HALVES, k=KS), multiply(n + i, 0, HALVES))
                 nc.vector.tensor_copy(
-                    out=y_group[:, i, 1:R, :].rearrange("p r (h w) -> p h r w", h=2),
-                    in_=y_group[:, i, 0, :].rearrange("p (h w) -> p h w", h=2).unsqueeze(2).to_broadcast([P, 2, R - 1, W // 2]),
+                    out=y_group[:, i, 1:R, :].rearrange("p r (h w) -> p h r w", h=HALVES),
+                    in_=first_copy.rearrange("p (h w) -> p h w", h=HALVES).unsqueeze(2).to_broadcast([P, HALVES, R - 1, WH]),
                 )
             nc.sync.dma_start(out=out_rows[:, n : n + size], in_=y_group[:])
             n += size

@@ -29,8 +29,8 @@ IDENTITY = mybir.ActivationFunctionType.Identity
 
 FLOPS = 2 * (L * C * C * KS + NL * 128 * C * W)
 
-CHUNKS = ((16, 2), (16, 2), (32, 2), (32, 2), (32, 2))
-WARM = (0, 0, 1, 1, 1)
+CHUNKS = ((32, 2), (32, 2), (32, 2), (32, 2))
+WARM = (0, 1, 1, 1)
 GROUPS = (2, 6, 7, 7)
 
 
@@ -115,21 +115,24 @@ def tile_conditionalfeaturesupsample_w4_kernel(
                 in_=grouped[:, T * c0 : T * (c0 + 64)],
             )
 
-        first_half = [c for c in range(len(CHUNKS)) if starts[c] < 64]
+        def scale_x():
+            nc.vector.tensor_tensor(
+                out=x_grouped[:],
+                in0=turned[:].rearrange("p t l -> p l t"),
+                in1=x_scale[:].unsqueeze(1).to_broadcast([P, L, T]),
+                op=MULT,
+            )
+
+        def quantize_x():
+            nc.vector.quantize_mx(
+                out=x_codes[:].bitcast(FP8X4), scales=x_scales[:], in_=x_grouped[:].rearrange("p l t -> p (l t)")
+            )
+
         second_half = [c for c in range(len(CHUNKS)) if starts[c] >= 64]
-        for c in first_half[:2]:
-            interleave(c)
-        nc.vector.tensor_tensor(
-            out=x_grouped[:],
-            in0=turned[:].rearrange("p t l -> p l t"),
-            in1=x_scale[:].unsqueeze(1).to_broadcast([P, L, T]),
-            op=MULT,
-        )
-        nc.vector.quantize_mx(
-            out=x_codes[:].bitcast(FP8X4), scales=x_scales[:], in_=x_grouped[:].rearrange("p l t -> p (l t)")
-        )
-        for c in first_half[2:]:
-            interleave(c)
+        interleave(0)
+        scale_x()
+        interleave(1)
+        quantize_x()
         for t in range(T):
             for k in range(KS):
                 quantize_w(k, t, 0)

@@ -180,11 +180,12 @@ def tile_conditionalfeaturesupsample_w4_kernel(
                     bias=bt_sb[:, t : t + 1],
                 )
 
-        def quantize_up(half):
+        def quantize_up(half, k0):
+            cols = slice(half * WH + k0 * LH, half * WH + (k0 + 2) * LH)
             nc.vector.quantize_mx(
-                out=up_codes[:, half * WH : (half + 1) * WH].bitcast(FP8X4),
-                scales=up_scales[:, half * WH : (half + 1) * WH],
-                in_=up_grouped[:, half].rearrange("p k l t -> p (k l t)"),
+                out=up_codes[:, cols].bitcast(FP8X4),
+                scales=up_scales[:, cols],
+                in_=up_grouped[:, half, k0 : k0 + 2].rearrange("p k l t -> p (k l t)"),
             )
 
         own = CHUNKS[-1][1]
@@ -235,13 +236,14 @@ def tile_conditionalfeaturesupsample_w4_kernel(
         add_bias_scalar(0, 1)
         for k in range(1, KS):
             add_bias(k, 0)
-        add_bias(1, 1)
-        quantize_up(0)
+        quantize_up(0, 0)
+        quantize_up(0, 2)
         first_layer(0)
         second_layer(0, empty_scalar)
-        add_bias(2, 1)
-        add_bias(3, 1)
-        quantize_up(1)
+        for k in range(1, KS):
+            add_bias(k, 1)
+        quantize_up(1, 0)
+        quantize_up(1, 2)
         first_layer(1)
         second_layer(1, empty_vector)
         nc.sync.dma_start(out=out_rows[:, 1], in_=y_second[:].rearrange("p r h l k -> p r (h l k)"))

@@ -30,6 +30,7 @@ IDENTITY = mybir.ActivationFunctionType.Identity
 FLOPS = 2 * (L * C * C * KS + NL * 128 * C * W)
 
 CHUNKS = ((32, 2), (32, 2), (32, 2), (32, 2))
+AHEAD = 3
 WARM = (0, 1, 1, 1)
 GROUPS = (2, 6, 7, 7)
 
@@ -190,10 +191,10 @@ def tile_conditionalfeaturesupsample_w4_kernel(
 
         own = CHUNKS[-1][1]
         for t in range(own):
-            for k in range(KS):
+            for k in range(AHEAD):
                 finish_w(k, t)
         for k in range(KS):
-            for t in range(own, T):
+            for t in range(own if k < AHEAD else 0, T):
                 finish_w(k, t)
 
         out_rows = out.rearrange("j b n (r w) -> j (b n) r w", r=R)
@@ -232,7 +233,7 @@ def tile_conditionalfeaturesupsample_w4_kernel(
             empty(1, y_second[:, :, half], multiply(1, half, half + 1)[:, 0].unsqueeze(1).to_broadcast([P, R, LH, KS]))
 
         nc.scalar.copy(out=b1_cols[:], in_=b1_turned[:])
-        add_bias(0, 0)
+        add_bias_scalar(0, 0)
         add_bias_scalar(0, 1)
         for k in range(1, KS):
             add_bias(k, 0)

@@ -32,7 +32,7 @@ FLOPS = 2 * (L * C * C * KS + NL * 128 * C * W)
 CHUNKS = ((32, 2), (32, 2), (32, 2), (32, 2))
 AHEAD = 3
 WARM = (0, 1, 1, 1)
-GROUPS = (2, 6, 7, 7)
+GROUPS = (2, 5, 7, 8)
 
 
 def tile_conditionalfeaturesupsample_w4_kernel(
@@ -88,7 +88,7 @@ def tile_conditionalfeaturesupsample_w4_kernel(
         x_codes = keep.tile([P, L], U32, align_bytes=64)
         x_scales = keep.tile([P, L], U8, align_bytes=64)
 
-        grouped = keep.tile([P, KS * T * P * T], BF16, align_bytes=64)
+        grouped = keep.tile([P, KS * T * P * T], BF16, align_bytes=64, tag="shared")
         grouped_v = grouped[:].rearrange("p (k t m j) -> p k t m j", k=KS, t=T, m=P)
         w_codes = keep.tile([P, KS * T * P], U32, align_bytes=64)
         w_scales = keep.tile([P, KS * T * P], U8, align_bytes=64)
@@ -216,9 +216,6 @@ def tile_conditionalfeaturesupsample_w4_kernel(
         def empty_scalar(n, dst, src):
             nc.scalar.activation(out=dst, in_=src, func=IDENTITY, bias=b1_cols[:, n : n + 1])
 
-        def empty_vector(n, dst, src):
-            nc.vector.tensor_scalar(out=dst, in0=src, scalar1=b1_cols[:, n : n + 1], scalar2=None, op0=ADD)
-
         def first_layer(half):
             y_half = keep.tile([P, WH], F32, tag=f"y_half_{half}")
             empty_scalar(0, y_half[:].rearrange("p (l k) -> p l k", k=KS), multiply(0, half, half + 1)[:, 0])
@@ -229,8 +226,14 @@ def tile_conditionalfeaturesupsample_w4_kernel(
 
         y_second = keep.tile([P, R, HALVES, LH, KS], F32)
 
-        def second_layer(half, empty):
-            empty(1, y_second[:, :, half], multiply(1, half, half + 1)[:, 0].unsqueeze(1).to_broadcast([P, R, LH, KS]))
+        def second_layer(half):
+            empty_scalar(1, y_second[:, 0, half], multiply(1, half, half + 1)[:, 0])
+
+        def repeat_second(half):
+            halves = y_second[:].rearrange("p r h (a l) k -> p h a r (l k)", a=2)
+            nc.vector.tensor_copy(
+                out=halves[:, half, :, 1:R], in_=halves[:, half, :, 0:1].to_broadcast([P, 2, R - 1, WH // 2])
+            )
 
         nc.scalar.copy(out=b1_cols[:], in_=b1_turned[:])
         add_bias_scalar(0, 0)
@@ -240,18 +243,20 @@ def tile_conditionalfeaturesupsample_w4_kernel(
         quantize_up(0, 0)
         quantize_up(0, 2)
         first_layer(0)
-        second_layer(0, empty_scalar)
+        second_layer(0)
         for k in range(1, KS):
             add_bias(k, 1)
         quantize_up(1, 0)
         quantize_up(1, 2)
         first_layer(1)
-        second_layer(1, empty_vector)
+        repeat_second(0)
+        second_layer(1)
+        repeat_second(1)
         nc.sync.dma_start(out=out_rows[:, 1], in_=y_second[:].rearrange("p r h l k -> p r (h l k)"))
 
         n = 2
         for size in GROUPS:
-            y_group = keep.tile([P, size, R, W], F32, tag="y_group", bufs=3)
+            y_group = keep.tile([P, size, R, W], F32, align_bytes=64, tag="shared" if n == 2 else f"y_group_{n}")
             for i in range(size):
                 first_copy = y_group[:, i, 0, :]
                 empty_scalar(n + i, first_copy.rearrange("p (h l k) -> p h l k", h=HALVES, k=KS), multiply(n + i, 0, HALVES))

@@ -49,6 +49,10 @@ def tile_conditionalfeaturesupsample_w4_kernel(
         x_scale = keep.tile([P, T], F32)
         nc.sync.dma_start(out=x_scale[:], in_=features_scale.rearrange("a b (p t) -> p (a b t)", t=T))
 
+        b1_rows = keep.tile([P, 128], BF16)
+        nc.vector.memset(b1_rows[0:64, :], 0.0)
+        b1_layers = b1.rearrange("(n j) -> n j", j=128)
+
         wt_rows = wt.rearrange("(p j) o k -> p j (o k)", j=T)
         raw = []
         starts = []
@@ -56,6 +60,9 @@ def tile_conditionalfeaturesupsample_w4_kernel(
         for c, (count, vector_slots) in enumerate(CHUNKS):
             raw_c = keep.tile([P, T, count * T * KS], BF16, align_bytes=64, tag=f"raw_{c}")
             nc.sync.dma_start(out=raw_c[:], in_=wt_rows[:, :, m0 * T * KS : (m0 + count) * T * KS])
+            if c == 0:
+                nc.sync.dma_start(out=b1_rows[0:16, :], in_=b1_layers[0:16, :])
+                nc.sync.dma_start(out=b1_rows[16:NL, :], in_=b1_layers[16:NL, :])
             raw.append(raw_c)
             starts.append(m0)
             m0 += count
@@ -67,9 +74,7 @@ def tile_conditionalfeaturesupsample_w4_kernel(
         w1_codes = keep.tile([P, 256 * NL], U8, align_bytes=64)
         w1_plane = keep.tile([P, 128 * NL], U8, align_bytes=64)
         nc.vector.memset(w1_plane[:].bitcast(I32), 0)
-        b1_rows = keep.tile([P, 128], BF16)
-        nc.scalar.activation(out=b1_rows[:], in_=ident[:], func=IDENTITY, scale=0.0)
-        nc.sync.dma_start(out=b1_rows[0:NL, :], in_=b1.rearrange("(n j) -> n j", j=128))
+        nc.scalar.activation(out=b1_rows[64:P, :], in_=ident[64:P, :], func=IDENTITY, scale=0.0)
 
         scale_rows = w1_scales.rearrange("g q n -> (g q) n").bitcast(I32)
         for quad in range(4):
@@ -99,11 +104,17 @@ def tile_conditionalfeaturesupsample_w4_kernel(
             count, vector_slots = CHUNKS[c]
             src = raw[c][:].rearrange("p j (m t k) -> p t m j k", t=T, k=KS)
             dst = grouped_v[:, :, :, starts[c] : starts[c] + count, :].rearrange("p k t m j -> p t m j k")
-            for t in range(T):
-                if t < vector_slots:
-                    nc.vector.tensor_copy(out=dst[:, t], in_=src[:, t])
-                else:
-                    nc.scalar.copy(out=dst[:, t], in_=src[:, t])
+            for t in range(vector_slots):
+                nc.vector.tensor_copy(out=dst[:, t], in_=src[:, t])
+            first_tap = 0
+            if c == len(CHUNKS) - 1:
+                nc.scalar.copy(
+                    out=dst[:, vector_slots:, :, :, 0].rearrange("p t m j -> p m j t"),
+                    in_=src[:, vector_slots:, :, :, 0].rearrange("p t m j -> p m j t"),
+                )
+                first_tap = 1
+            for t in range(vector_slots, T):
+                nc.scalar.copy(out=dst[:, t, :, :, first_tap:], in_=src[:, t, :, :, first_tap:])
             for i in range(WARM[c]):
                 words = raw[c][:].rearrange("p j n -> p (j n)").bitcast(F32)
                 nc.tensor.matmul(warm[:], lhsT=words[:, 0:P], rhs=words[:, 0:256], start=True, stop=True)
@@ -132,6 +143,10 @@ def tile_conditionalfeaturesupsample_w4_kernel(
         second_half = [c for c in range(len(CHUNKS)) if starts[c] >= 64]
         interleave(0)
         scale_x()
+        b1_turned = psum.tile([P, NL], F32, tag="acc")
+        nc.tensor.matmul(b1_turned[:], lhsT=b1_rows[:], rhs=ident[:, 0:NL], start=True, stop=True)
+        b1_cols = keep.tile([P, NL], F32)
+        nc.vector.tensor_copy(out=b1_cols[:], in_=b1_turned[:])
         interleave(1)
         quantize_x()
         for t in range(T):
@@ -139,9 +154,6 @@ def tile_conditionalfeaturesupsample_w4_kernel(
                 quantize_w(k, t, 0)
         for c in second_half:
             interleave(c)
-
-        b1_turned = psum.tile([P, NL], F32, tag="turn", bufs=1)
-        nc.tensor.matmul(b1_turned[:], lhsT=b1_rows[:], rhs=ident[:, 0:NL], start=True, stop=True)
 
         up_grouped = keep.tile([P, HALVES, KS, LH, T], BF16, align_bytes=64)
         up_codes = keep.tile([P, W], U32, align_bytes=64)
@@ -181,36 +193,40 @@ def tile_conditionalfeaturesupsample_w4_kernel(
                     bias=bt_sb[:, t : t + 1],
                 )
 
-        def quantize_up(half, k0):
-            cols = slice(half * WH + k0 * LH, half * WH + (k0 + 2) * LH)
+        def quantize_up(half, k0, k1):
+            cols = slice(half * WH + k0 * LH, half * WH + k1 * LH)
             nc.vector.quantize_mx(
                 out=up_codes[:, cols].bitcast(FP8X4),
                 scales=up_scales[:, cols],
-                in_=up_grouped[:, half, k0 : k0 + 2].rearrange("p k l t -> p (k l t)"),
+                in_=up_grouped[:, half, k0:k1].rearrange("p k l t -> p (k l t)"),
             )
 
         own = CHUNKS[-1][1]
+        for t in range(T):
+            finish_w(0, t)
         for t in range(own):
-            for k in range(AHEAD):
+            for k in range(1, AHEAD):
                 finish_w(k, t)
-        for k in range(KS):
+        for k in range(1, KS):
             for t in range(own if k < AHEAD else 0, T):
                 finish_w(k, t)
 
         out_rows = out.rearrange("j b n (r w) -> j (b n) r w", r=R)
-        b1_cols = keep.tile([P, NL], F32)
 
-        def multiply(n, h0, h1):
+        def multiply(n, h0, h1, passes=1):
             acc = psum.tile([P, h1 - h0, KS, LH], F32, tag="acc")
-            nc.tensor.matmul_mx(
-                out=acc[:].rearrange("p h k l -> p (h k l)"),
-                lhsT=w1_codes[:, 256 * n : 256 * (n + 1)].bitcast(FP4X4),
-                lhsT_scale=w1_plane[:, 128 * n : 128 * (n + 1)],
-                rhs=up_codes[:, h0 * WH : h1 * WH].bitcast(FP8X4),
-                rhs_scale=up_scales[:, h0 * WH : h1 * WH],
-                start=True,
-                stop=True,
-            )
+            width = (h1 - h0) * WH // passes
+            for c0 in range(0, (h1 - h0) * WH, width):
+                cols = slice(h0 * WH + c0, h0 * WH + c0 + width)
+                nc.tensor.matmul_mx(
+                    out=acc[:].rearrange("p h k l -> p (h k l)")[:, c0 : c0 + width],
+                    lhsT=w1_codes[:, 256 * n : 256 * (n + 1)].bitcast(FP4X4),
+                    lhsT_scale=w1_plane[:, 128 * n : 128 * (n + 1)],
+                    rhs=up_codes[:, cols].bitcast(FP8X4),
+                    rhs_scale=up_scales[:, cols],
+                    start=True,
+                    stop=True,
+                )
             return acc[:].rearrange("p h k l -> p h l k")
 
         def empty_scalar(n, dst, src):
@@ -218,7 +234,7 @@ def tile_conditionalfeaturesupsample_w4_kernel(
 
         def first_layer(half):
             y_half = keep.tile([P, WH], F32, tag=f"y_half_{half}")
-            empty_scalar(0, y_half[:].rearrange("p (l k) -> p l k", k=KS), multiply(0, half, half + 1)[:, 0])
+            empty_scalar(0, y_half[:].rearrange("p (l k) -> p l k", k=KS), multiply(0, half, half + 1, passes=2)[:, 0])
             nc.sync.dma_start(
                 out=out_rows[:, 0, :, half * WH : (half + 1) * WH],
                 in_=y_half[:].unsqueeze(1).to_broadcast([P, R, WH]),
@@ -235,19 +251,20 @@ def tile_conditionalfeaturesupsample_w4_kernel(
                 out=halves[:, half, :, 1:R], in_=halves[:, half, :, 0:1].to_broadcast([P, 2, R - 1, WH // 2])
             )
 
-        nc.scalar.copy(out=b1_cols[:], in_=b1_turned[:])
         add_bias_scalar(0, 0)
         add_bias_scalar(0, 1)
         for k in range(1, KS):
             add_bias(k, 0)
-        quantize_up(0, 0)
-        quantize_up(0, 2)
+        quantize_up(0, 0, 2)
+        quantize_up(0, 2, 3)
+        quantize_up(0, 3, 4)
         first_layer(0)
         second_layer(0)
         for k in range(1, KS):
             add_bias(k, 1)
-        quantize_up(1, 0)
-        quantize_up(1, 2)
+        quantize_up(1, 0, 2)
+        quantize_up(1, 2, 3)
+        quantize_up(1, 3, 4)
         first_layer(1)
         repeat_second(0)
         second_layer(1)

@@ -252,7 +252,6 @@ def tile_conditionalfeaturesupsample_w4_kernel(
             )
 
         add_bias_scalar(0, 0)
-        add_bias_scalar(0, 1)
         for k in range(1, KS):
             add_bias(k, 0)
         quantize_up(0, 0, 2)
@@ -260,7 +259,7 @@ def tile_conditionalfeaturesupsample_w4_kernel(
         quantize_up(0, 3, 4)
         first_layer(0)
         second_layer(0)
-        for k in range(1, KS):
+        for k in range(KS):
             add_bias(k, 1)
         quantize_up(1, 0, 2)
         quantize_up(1, 2, 3)

@@ -30,7 +30,7 @@ IDENTITY = mybir.ActivationFunctionType.Identity
 FLOPS = 2 * (L * C * C * KS + NL * 128 * C * W)
 
 CHUNKS = ((32, 2), (32, 2), (32, 2), (32, 2))
-AHEAD = 3
+SPLIT = 16
 WARM = (0, 1, 1, 1)
 GROUPS = (2, 5, 7, 8)
 
@@ -104,17 +104,19 @@ def tile_conditionalfeaturesupsample_w4_kernel(
             count, vector_slots = CHUNKS[c]
             src = raw[c][:].rearrange("p j (m t k) -> p t m j k", t=T, k=KS)
             dst = grouped_v[:, :, :, starts[c] : starts[c] + count, :].rearrange("p k t m j -> p t m j k")
-            for t in range(vector_slots):
-                nc.vector.tensor_copy(out=dst[:, t], in_=src[:, t])
-            first_tap = 0
-            if c == len(CHUNKS) - 1:
-                nc.scalar.copy(
-                    out=dst[:, vector_slots:, :, :, 0].rearrange("p t m j -> p m j t"),
-                    in_=src[:, vector_slots:, :, :, 0].rearrange("p t m j -> p m j t"),
-                )
-                first_tap = 1
-            for t in range(vector_slots, T):
-                nc.scalar.copy(out=dst[:, t, :, :, first_tap:], in_=src[:, t, :, :, first_tap:])
+            if c < len(CHUNKS) - 1:
+                for t in range(vector_slots):
+                    nc.vector.tensor_copy(out=dst[:, t], in_=src[:, t])
+                for t in range(vector_slots, T):
+                    nc.scalar.copy(out=dst[:, t], in_=src[:, t])
+            else:
+                nc.vector.tensor_copy(out=dst[:, 0], in_=src[:, 0])
+                nc.vector.tensor_copy(out=dst[:, 1, :SPLIT], in_=src[:, 1, :SPLIT])
+                src_pair = src[:, 2:T].rearrange("p t m j k -> p m j t k")
+                dst_pair = dst[:, 2:T].rearrange("p t m j k -> p m j t k")
+                nc.scalar.copy(out=dst_pair[:, :, :, :, 0:2], in_=src_pair[:, :, :, :, 0:2])
+                nc.scalar.copy(out=dst[:, 1, SPLIT:], in_=src[:, 1, SPLIT:])
+                nc.scalar.copy(out=dst_pair[:, :, :, :, 2:KS], in_=src_pair[:, :, :, :, 2:KS])
             for i in range(WARM[c]):
                 words = raw[c][:].rearrange("p j n -> p (j n)").bitcast(F32)
                 nc.tensor.matmul(warm[:], lhsT=words[:, 0:P], rhs=words[:, 0:256], start=True, stop=True)
@@ -201,15 +203,12 @@ def tile_conditionalfeaturesupsample_w4_kernel(
                 in_=up_grouped[:, half, k0:k1].rearrange("p k l t -> p (k l t)"),
             )
 
-        own = CHUNKS[-1][1]
-        for t in range(T):
-            finish_w(0, t)
-        for t in range(own):
-            for k in range(1, AHEAD):
-                finish_w(k, t)
-        for k in range(1, KS):
-            for t in range(own if k < AHEAD else 0, T):
-                finish_w(k, t)
+        for k, t in ((0, 0), (0, 2), (0, 3), (1, 0), (0, 1), (1, 1), (1, 2), (1, 3)):
+            finish_w(k, t)
+        for slots in ((0, 1), (2, 3)):
+            for k in (2, 3):
+                for t in slots:
+                    finish_w(k, t)
 
         out_rows = out.rearrange("j b n (r w) -> j (b n) r w", r=R)
 

@@ -186,14 +186,22 @@ def tile_conditionalfeaturesupsample_w4_kernel(
                 op=ADD,
             )
 
-        def add_bias_scalar(k, half):
+        up_rows = []
+        for k in range(KS - 1):
+            rows_k = keep.tile([P, T, L], BF16, align_bytes=64, tag=f"up_rows_{k}")
+            up_rows.append(rows_k)
+
+        def empty_rows(k, l0, l1):
             for t in range(T):
                 nc.scalar.activation(
-                    out=up_grouped[:, half, k, :, t],
-                    in_=up_acc[k][:, t, half * LH : (half + 1) * LH],
-                    func=IDENTITY,
-                    bias=bt_sb[:, t : t + 1],
+                    out=up_rows[k][:, t, l0:l1], in_=up_acc[k][:, t, l0:l1], func=IDENTITY, bias=bt_sb[:, t : t + 1]
                 )
+
+        def weave(k, half):
+            nc.vector.tensor_copy(
+                out=up_grouped[:, half, k].rearrange("p (c i) t -> p c t i", i=4),
+                in_=up_rows[k][:, :, half * LH : (half + 1) * LH].rearrange("p t (c i) -> p c t i", i=4),
+            )
 
         def quantize_up(half, k0, k1):
             cols = slice(half * WH + k0 * LH, half * WH + k1 * LH)
@@ -212,10 +220,10 @@ def tile_conditionalfeaturesupsample_w4_kernel(
 
         out_rows = out.rearrange("j b n (r w) -> j (b n) r w", r=R)
 
-        def multiply(n, h0, h1, passes=1):
+        def multiply(n, h0, h1, passes=1, backwards=False):
             acc = psum.tile([P, h1 - h0, KS, LH], F32, tag="acc")
             width = (h1 - h0) * WH // passes
-            for c0 in range(0, (h1 - h0) * WH, width):
+            for c0 in sorted(range(0, (h1 - h0) * WH, width), reverse=backwards):
                 cols = slice(h0 * WH + c0, h0 * WH + c0 + width)
                 nc.tensor.matmul_mx(
                     out=acc[:].rearrange("p h k l -> p (h k l)")[:, c0 : c0 + width],
@@ -233,7 +241,7 @@ def tile_conditionalfeaturesupsample_w4_kernel(
 
         def first_layer(half):
             y_half = keep.tile([P, WH], F32, tag=f"y_half_{half}")
-            empty_scalar(0, y_half[:].rearrange("p (l k) -> p l k", k=KS), multiply(0, half, half + 1, passes=2)[:, 0])
+            empty_scalar(0, y_half[:].rearrange("p (l k) -> p l k", k=KS), multiply(0, half, half + 1, passes=2, backwards=half == 1)[:, 0])
             nc.sync.dma_start(
                 out=out_rows[:, 0, :, half * WH : (half + 1) * WH],
                 in_=y_half[:].unsqueeze(1).to_broadcast([P, R, WH]),
@@ -250,19 +258,24 @@ def tile_conditionalfeaturesupsample_w4_kernel(
                 out=halves[:, half, :, 1:R], in_=halves[:, half, :, 0:1].to_broadcast([P, 2, R - 1, WH // 2])
             )
 
-        add_bias_scalar(0, 0)
-        for k in range(1, KS):
-            add_bias(k, 0)
+        empty_rows(0, 0, L)
+        add_bias(1, 0)
+        add_bias(2, 0)
+        weave(0, 0)
+        add_bias(3, 0)
+        empty_rows(1, LH, L)
+        empty_rows(2, LH, L)
         quantize_up(0, 0, 2)
         quantize_up(0, 2, 3)
         quantize_up(0, 3, 4)
         first_layer(0)
         second_layer(0)
-        for k in range(KS):
-            add_bias(k, 1)
+        add_bias(3, 1)
+        weave(2, 1)
+        weave(0, 1)
+        weave(1, 1)
+        quantize_up(1, 2, 4)
         quantize_up(1, 0, 2)
-        quantize_up(1, 2, 3)
-        quantize_up(1, 3, 4)
         first_layer(1)
         repeat_second(0)
         second_layer(1)

@@ -131,9 +131,9 @@ def tile_conditionalfeaturesupsample_w4_kernel(
 
         def scale_x():
             nc.vector.tensor_tensor(
-                out=x_grouped[:],
-                in0=turned[:].rearrange("p t l -> p l t"),
-                in1=x_scale[:].unsqueeze(1).to_broadcast([P, L, T]),
+                out=x_grouped[:].rearrange("p (c i) t -> p c t i", i=2),
+                in0=turned[:].rearrange("p t (c i) -> p c t i", i=2),
+                in1=x_scale[:].unsqueeze(1).unsqueeze(3).to_broadcast([P, L // 2, T, 2]),
                 op=MULT,
             )
 
@@ -180,9 +180,9 @@ def tile_conditionalfeaturesupsample_w4_kernel(
 
         def add_bias(k, half):
             nc.vector.tensor_tensor(
-                out=up_grouped[:, half, k],
-                in0=up_acc[k][:, :, half * LH : (half + 1) * LH].rearrange("p t l -> p l t"),
-                in1=bt_sb[:].unsqueeze(1).to_broadcast([P, LH, T]),
+                out=up_grouped[:, half, k].rearrange("p (c i) t -> p c t i", i=2),
+                in0=up_acc[k][:, :, half * LH : (half + 1) * LH].rearrange("p t (c i) -> p c t i", i=2),
+                in1=bt_sb[:].unsqueeze(1).unsqueeze(3).to_broadcast([P, LH // 2, T, 2]),
                 op=ADD,
             )
 

@@ -31,8 +31,11 @@ FLOPS = 2 * (L * C * C * KS + NL * 128 * C * W)
 
 CHUNKS = ((32, 2), (32, 2), (32, 2), (32, 2))
 SPLIT = 16
+B1_ROWS = 8
+B1_SIDE = NL // B1_ROWS
+ROW_TAPS = 2
 WARM = (0, 1, 1, 1)
-GROUPS = (2, 5, 7, 8)
+GROUPS = (3, 5, 7, 7)
 
 
 def tile_conditionalfeaturesupsample_w4_kernel(
@@ -44,37 +47,37 @@ def tile_conditionalfeaturesupsample_w4_kernel(
         psum = ctx.enter_context(tc.psum_pool(name="psum", bufs=7))
         ctx.enter_context(tc.manual_schedule())
 
-        x_bytes = keep.tile([P, C], U8, align_bytes=64)
+        x_bytes = keep.tile([P, C], U8, align_bytes=256)
         nc.sync.dma_start(out=x_bytes[:], in_=features_bytes.rearrange("b l c -> (b l) c"))
         x_scale = keep.tile([P, T], F32)
-        nc.sync.dma_start(out=x_scale[:], in_=features_scale.rearrange("a b (p t) -> p (a b t)", t=T))
 
-        b1_rows = keep.tile([P, 128], BF16)
-        nc.vector.memset(b1_rows[0:64, :], 0.0)
-        b1_layers = b1.rearrange("(n j) -> n j", j=128)
+        b1_rows = keep.tile([P, B1_SIDE, 128], BF16, align_bytes=256)
+        nc.vector.memset(b1_rows[0:64], 0.0)
 
         wt_rows = wt.rearrange("(p j) o k -> p j (o k)", j=T)
         raw = []
         starts = []
         m0 = 0
         for c, (count, vector_slots) in enumerate(CHUNKS):
-            raw_c = keep.tile([P, T, count * T * KS], BF16, align_bytes=64, tag=f"raw_{c}")
+            raw_c = keep.tile([P, T, count * T * KS], BF16, align_bytes=256, tag=f"raw_{c}")
             nc.sync.dma_start(out=raw_c[:], in_=wt_rows[:, :, m0 * T * KS : (m0 + count) * T * KS])
             if c == 0:
-                nc.sync.dma_start(out=b1_rows[0:16, :], in_=b1_layers[0:16, :])
-                nc.sync.dma_start(out=b1_rows[16:NL, :], in_=b1_layers[16:NL, :])
+                nc.sync.dma_start(out=x_scale[:], in_=features_scale.rearrange("a b (p t) -> p (a b t)", t=T))
             raw.append(raw_c)
             starts.append(m0)
             m0 += count
         bt_sb = keep.tile([P, T], BF16)
         nc.sync.dma_start(out=bt_sb[:], in_=bt.rearrange("(p t) -> p t", t=T))
+        nc.sync.dma_start(out=b1_rows[0:B1_ROWS], in_=b1.rearrange("(q i j) -> q i j", i=B1_SIDE, j=128))
 
         ident = keep.tile([P, P], BF16)
         make_identity(nc, ident[:])
-        w1_codes = keep.tile([P, 256 * NL], U8, align_bytes=64)
-        w1_plane = keep.tile([P, 128 * NL], U8, align_bytes=64)
+        w1_codes = keep.tile([P, 256 * NL], U8, align_bytes=256)
+        w1_plane = keep.tile([P, 128 * NL], U8, align_bytes=256)
         nc.vector.memset(w1_plane[:].bitcast(I32), 0)
-        nc.scalar.activation(out=b1_rows[64:P, :], in_=ident[64:P, :], func=IDENTITY, scale=0.0)
+        nc.scalar.activation(
+            out=b1_rows[64:P], in_=ident[64:P, :].unsqueeze(1).to_broadcast([64, B1_SIDE, P]), func=IDENTITY, scale=0.0
+        )
 
         scale_rows = w1_scales.rearrange("g q n -> (g q) n").bitcast(I32)
         for quad in range(4):
@@ -93,20 +96,22 @@ def tile_conditionalfeaturesupsample_w4_kernel(
         x_codes = keep.tile([P, L], U32, align_bytes=64)
         x_scales = keep.tile([P, L], U8, align_bytes=64)
 
-        grouped = keep.tile([P, KS * T * P * T], BF16, align_bytes=64, tag="shared")
+        grouped = keep.tile([P, KS * T * P * T], BF16, align_bytes=256, tag="shared")
         grouped_v = grouped[:].rearrange("p (k t m j) -> p k t m j", k=KS, t=T, m=P)
         w_codes = keep.tile([P, KS * T * P], U32, align_bytes=64)
         w_scales = keep.tile([P, KS * T * P], U8, align_bytes=64)
 
         warm = psum.tile([P, 256], F32, tag="acc")
 
-        def interleave(c):
+        def interleave(c, between=None):
             count, vector_slots = CHUNKS[c]
             src = raw[c][:].rearrange("p j (m t k) -> p t m j k", t=T, k=KS)
             dst = grouped_v[:, :, :, starts[c] : starts[c] + count, :].rearrange("p k t m j -> p t m j k")
             if c < len(CHUNKS) - 1:
                 for t in range(vector_slots):
                     nc.vector.tensor_copy(out=dst[:, t], in_=src[:, t])
+                    if between and t == 0:
+                        between()
                 for t in range(vector_slots, T):
                     nc.scalar.copy(out=dst[:, t], in_=src[:, t])
             else:
@@ -116,7 +121,8 @@ def tile_conditionalfeaturesupsample_w4_kernel(
                 dst_pair = dst[:, 2:T].rearrange("p t m j k -> p m j t k")
                 nc.scalar.copy(out=dst_pair[:, :, :, :, 0:2], in_=src_pair[:, :, :, :, 0:2])
                 nc.scalar.copy(out=dst[:, 1, SPLIT:], in_=src[:, 1, SPLIT:])
-                nc.scalar.copy(out=dst_pair[:, :, :, :, 2:KS], in_=src_pair[:, :, :, :, 2:KS])
+                for k in (2, 3):
+                    nc.scalar.copy(out=dst_pair[:, :, :, :, k], in_=src_pair[:, :, :, :, k])
             for i in range(WARM[c]):
                 words = raw[c][:].rearrange("p j n -> p (j n)").bitcast(F32)
                 nc.tensor.matmul(warm[:], lhsT=words[:, 0:P], rhs=words[:, 0:256], start=True, stop=True)
@@ -131,9 +137,9 @@ def tile_conditionalfeaturesupsample_w4_kernel(
 
         def scale_x():
             nc.vector.tensor_tensor(
-                out=x_grouped[:].rearrange("p (c i) t -> p c t i", i=2),
-                in0=turned[:].rearrange("p t (c i) -> p c t i", i=2),
-                in1=x_scale[:].unsqueeze(1).unsqueeze(3).to_broadcast([P, L // 2, T, 2]),
+                out=x_grouped[:],
+                in0=turned[:].rearrange("p t l -> p l t"),
+                in1=x_scale[:].unsqueeze(1).to_broadcast([P, L, T]),
                 op=MULT,
             )
 
@@ -143,14 +149,9 @@ def tile_conditionalfeaturesupsample_w4_kernel(
             )
 
         second_half = [c for c in range(len(CHUNKS)) if starts[c] >= 64]
-        interleave(0)
-        scale_x()
-        b1_turned = psum.tile([P, NL], F32, tag="acc")
-        nc.tensor.matmul(b1_turned[:], lhsT=b1_rows[:], rhs=ident[:, 0:NL], start=True, stop=True)
-        b1_cols = keep.tile([P, NL], F32)
-        nc.vector.tensor_copy(out=b1_cols[:], in_=b1_turned[:])
-        interleave(1)
+        interleave(0, between=scale_x)
         quantize_x()
+        interleave(1)
         for t in range(T):
             for k in range(KS):
                 quantize_w(k, t, 0)
@@ -180,27 +181,36 @@ def tile_conditionalfeaturesupsample_w4_kernel(
 
         def add_bias(k, half):
             nc.vector.tensor_tensor(
-                out=up_grouped[:, half, k].rearrange("p (c i) t -> p c t i", i=2),
-                in0=up_acc[k][:, :, half * LH : (half + 1) * LH].rearrange("p t (c i) -> p c t i", i=2),
-                in1=bt_sb[:].unsqueeze(1).unsqueeze(3).to_broadcast([P, LH // 2, T, 2]),
+                out=up_grouped[:, half, k],
+                in0=up_acc[k][:, :, half * LH : (half + 1) * LH].rearrange("p t l -> p l t"),
+                in1=bt_sb[:].unsqueeze(1).to_broadcast([P, LH, T]),
                 op=ADD,
             )
 
-        up_rows = []
-        for k in range(KS - 1):
-            rows_k = keep.tile([P, T, L], BF16, align_bytes=64, tag=f"up_rows_{k}")
-            up_rows.append(rows_k)
-
-        def empty_rows(k, l0, l1):
+        def add_bias_scalar(k, half):
             for t in range(T):
                 nc.scalar.activation(
-                    out=up_rows[k][:, t, l0:l1], in_=up_acc[k][:, t, l0:l1], func=IDENTITY, bias=bt_sb[:, t : t + 1]
+                    out=up_grouped[:, half, k, :, t],
+                    in_=up_acc[k][:, t, half * LH : (half + 1) * LH],
+                    func=IDENTITY,
+                    bias=bt_sb[:, t : t + 1],
                 )
 
-        def weave(k, half):
+        up_rows = []
+        for k in range(ROW_TAPS):
+            rows_k = keep.tile([P, T, LH], BF16, align_bytes=64, tag=f"up_rows_{k}")
+            up_rows.append(rows_k)
+
+        def empty_rows(k):
+            for t in range(T):
+                nc.scalar.activation(
+                    out=up_rows[k][:, t, :], in_=up_acc[k][:, t, LH:L], func=IDENTITY, bias=bt_sb[:, t : t + 1]
+                )
+
+        def weave(k):
             nc.vector.tensor_copy(
-                out=up_grouped[:, half, k].rearrange("p (c i) t -> p c t i", i=4),
-                in_=up_rows[k][:, :, half * LH : (half + 1) * LH].rearrange("p t (c i) -> p c t i", i=4),
+                out=up_grouped[:, 1, k].rearrange("p (c i) t -> p c t i", i=4),
+                in_=up_rows[k][:].rearrange("p t (c i) -> p c t i", i=4),
             )
 
         def quantize_up(half, k0, k1):
@@ -218,12 +228,17 @@ def tile_conditionalfeaturesupsample_w4_kernel(
                 for t in slots:
                     finish_w(k, t)
 
+        b1_turned = psum.tile([P, B1_SIDE, B1_ROWS], F32, tag="acc")
+        for i in range(B1_SIDE):
+            nc.tensor.matmul(b1_turned[:, i, :], lhsT=b1_rows[:, i, :], rhs=ident[:, 0:B1_ROWS], start=True, stop=True)
+        b1_cols = keep.tile([P, B1_ROWS, B1_SIDE], F32)
+
         out_rows = out.rearrange("j b n (r w) -> j (b n) r w", r=R)
 
-        def multiply(n, h0, h1, passes=1, backwards=False):
+        def multiply(n, h0, h1, passes=1):
             acc = psum.tile([P, h1 - h0, KS, LH], F32, tag="acc")
             width = (h1 - h0) * WH // passes
-            for c0 in sorted(range(0, (h1 - h0) * WH, width), reverse=backwards):
+            for c0 in range(0, (h1 - h0) * WH, width):
                 cols = slice(h0 * WH + c0, h0 * WH + c0 + width)
                 nc.tensor.matmul_mx(
                     out=acc[:].rearrange("p h k l -> p (h k l)")[:, c0 : c0 + width],
@@ -237,54 +252,55 @@ def tile_conditionalfeaturesupsample_w4_kernel(
             return acc[:].rearrange("p h k l -> p h l k")
 
         def empty_scalar(n, dst, src):
-            nc.scalar.activation(out=dst, in_=src, func=IDENTITY, bias=b1_cols[:, n : n + 1])
+            nc.scalar.activation(out=dst, in_=src, func=IDENTITY, bias=b1_cols[:].rearrange("p q i -> p (q i)")[:, n : n + 1])
 
-        def first_layer(half):
-            y_half = keep.tile([P, WH], F32, tag=f"y_half_{half}")
-            empty_scalar(0, y_half[:].rearrange("p (l k) -> p l k", k=KS), multiply(0, half, half + 1, passes=2, backwards=half == 1)[:, 0])
+        y_first = keep.tile([P, WH], F32, align_bytes=256)
+        y_joined = keep.tile([P, WH + R * W], F32, align_bytes=256)
+        y_second = y_joined[:, WH:].rearrange("p (r h l k) -> p r h l k", r=R, h=HALVES, k=KS)
+
+        def first_layer(half, y_half, copies):
+            empty_scalar(0, y_half.rearrange("p (l k) -> p l k", k=KS), multiply(0, half, half + 1, passes=2)[:, 0])
             nc.sync.dma_start(
-                out=out_rows[:, 0, :, half * WH : (half + 1) * WH],
-                in_=y_half[:].unsqueeze(1).to_broadcast([P, R, WH]),
+                out=out_rows[:, 0, 0:copies, half * WH : (half + 1) * WH],
+                in_=y_half.unsqueeze(1).to_broadcast([P, copies, WH]),
             )
-
-        y_second = keep.tile([P, R, HALVES, LH, KS], F32)
 
         def second_layer(half):
             empty_scalar(1, y_second[:, 0, half], multiply(1, half, half + 1)[:, 0])
 
         def repeat_second(half):
-            halves = y_second[:].rearrange("p r h (a l) k -> p h a r (l k)", a=2)
+            halves = y_second.rearrange("p r h (a l) k -> p h a r (l k)", a=2)
             nc.vector.tensor_copy(
                 out=halves[:, half, :, 1:R], in_=halves[:, half, :, 0:1].to_broadcast([P, 2, R - 1, WH // 2])
             )
 
-        empty_rows(0, 0, L)
-        add_bias(1, 0)
-        add_bias(2, 0)
-        weave(0, 0)
-        add_bias(3, 0)
-        empty_rows(1, LH, L)
-        empty_rows(2, LH, L)
+        add_bias_scalar(0, 0)
+        nc.scalar.copy(out=b1_cols[:], in_=b1_turned[:].rearrange("p i q -> p q i"))
+        for k in range(1, KS):
+            add_bias(k, 0)
+        for k in range(ROW_TAPS):
+            empty_rows(k)
         quantize_up(0, 0, 2)
         quantize_up(0, 2, 3)
         quantize_up(0, 3, 4)
-        first_layer(0)
+        first_layer(0, y_first[:], R)
         second_layer(0)
-        add_bias(3, 1)
-        weave(2, 1)
-        weave(0, 1)
-        weave(1, 1)
-        quantize_up(1, 2, 4)
+        for k in range(ROW_TAPS):
+            weave(k)
+        for k in range(ROW_TAPS, KS):
+            add_bias(k, 1)
         quantize_up(1, 0, 2)
-        first_layer(1)
+        quantize_up(1, 2, 3)
+        quantize_up(1, 3, 4)
+        first_layer(1, y_joined[:, 0:WH], R - 1)
         repeat_second(0)
         second_layer(1)
         repeat_second(1)
-        nc.sync.dma_start(out=out_rows[:, 1], in_=y_second[:].rearrange("p r h l k -> p r (h l k)"))
+        nc.sync.dma_start(out=out.rearrange("j b n w -> j (b n w)")[:, R * W - WH : 2 * R * W], in_=y_joined[:])
 
         n = 2
         for size in GROUPS:
-            y_group = keep.tile([P, size, R, W], F32, align_bytes=64, tag="shared" if n == 2 else f"y_group_{n}")
+            y_group = keep.tile([P, size, R, W], F32, align_bytes=256, tag="shared" if n == 2 else f"y_group_{n}")
             for i in range(size):
                 first_copy = y_group[:, i, 0, :]
                 empty_scalar(n + i, first_copy.rearrange("p (h l k) -> p h l k", h=HALVES, k=KS), multiply(n + i, 0, HALVES))

@@ -33,7 +33,7 @@ CHUNKS = ((32, 2), (32, 2), (32, 2), (32, 2))
 SPLIT = 16
 B1_ROWS = 8
 B1_SIDE = NL // B1_ROWS
-ROW_TAPS = 2
+ROW_TAPS = 1
 WARM = (0, 1, 1, 1)
 GROUPS = (3, 5, 7, 7)
 
@@ -115,7 +115,8 @@ def tile_conditionalfeaturesupsample_w4_kernel(
                 for t in range(vector_slots, T):
                     nc.scalar.copy(out=dst[:, t], in_=src[:, t])
             else:
-                nc.vector.tensor_copy(out=dst[:, 0], in_=src[:, 0])
+                nc.vector.tensor_copy(out=dst[:, 0, :, :, 0:2], in_=src[:, 0, :, :, 0:2])
+                nc.vector.tensor_copy(out=dst[:, 0, :, :, 2:KS], in_=src[:, 0, :, :, 2:KS])
                 nc.vector.tensor_copy(out=dst[:, 1, :SPLIT], in_=src[:, 1, :SPLIT])
                 src_pair = src[:, 2:T].rearrange("p t m j k -> p m j t k")
                 dst_pair = dst[:, 2:T].rearrange("p t m j k -> p m j t k")
@@ -275,11 +276,11 @@ def tile_conditionalfeaturesupsample_w4_kernel(
             )
 
         add_bias_scalar(0, 0)
-        nc.scalar.copy(out=b1_cols[:], in_=b1_turned[:].rearrange("p i q -> p q i"))
         for k in range(1, KS):
             add_bias(k, 0)
         for k in range(ROW_TAPS):
             empty_rows(k)
+        nc.scalar.copy(out=b1_cols[:], in_=b1_turned[:].rearrange("p i q -> p q i"))
         quantize_up(0, 0, 2)
         quantize_up(0, 2, 3)
         quantize_up(0, 3, 4)

@@ -33,9 +33,9 @@ CHUNKS = ((32, 2), (32, 2), (32, 2), (32, 2))
 SPLIT = 16
 B1_ROWS = 8
 B1_SIDE = NL // B1_ROWS
-ROW_TAPS = 1
+ROW_TAPS = 2
 WARM = (0, 1, 1, 1)
-GROUPS = (3, 5, 7, 7)
+GROUPS = (2, 5, 7, 8)
 
 
 def tile_conditionalfeaturesupsample_w4_kernel(

@@ -259,9 +259,9 @@ def tile_conditionalfeaturesupsample_w4_kernel(
         y_joined = keep.tile([P, WH + R * W], F32, align_bytes=256)
         y_second = y_joined[:, WH:].rearrange("p (r h l k) -> p r h l k", r=R, h=HALVES, k=KS)
 
-        def first_layer(half, y_half, copies):
+        def first_layer(half, y_half, copies, queue):
             empty_scalar(0, y_half.rearrange("p (l k) -> p l k", k=KS), multiply(0, half, half + 1, passes=2)[:, 0])
-            nc.sync.dma_start(
+            queue.dma_start(
                 out=out_rows[:, 0, 0:copies, half * WH : (half + 1) * WH],
                 in_=y_half.unsqueeze(1).to_broadcast([P, copies, WH]),
             )
@@ -284,7 +284,7 @@ def tile_conditionalfeaturesupsample_w4_kernel(
         quantize_up(0, 0, 2)
         quantize_up(0, 2, 3)
         quantize_up(0, 3, 4)
-        first_layer(0, y_first[:], R)
+        first_layer(0, y_first[:], R, nc.scalar)
         second_layer(0)
         for k in range(ROW_TAPS):
             weave(k)
@@ -293,7 +293,7 @@ def tile_conditionalfeaturesupsample_w4_kernel(
         quantize_up(1, 0, 2)
         quantize_up(1, 2, 3)
         quantize_up(1, 3, 4)
-        first_layer(1, y_joined[:, 0:WH], R - 1)
+        first_layer(1, y_joined[:, 0:WH], R - 1, nc.sync)
         repeat_second(0)
         second_layer(1)
         repeat_second(1)

@@ -259,8 +259,10 @@ def tile_conditionalfeaturesupsample_w4_kernel(
         y_joined = keep.tile([P, WH + R * W], F32, align_bytes=256)
         y_second = y_joined[:, WH:].rearrange("p (r h l k) -> p r h l k", r=R, h=HALVES, k=KS)
 
-        def first_layer(half, y_half, copies, queue):
+        def first_layer(half, y_half):
             empty_scalar(0, y_half.rearrange("p (l k) -> p l k", k=KS), multiply(0, half, half + 1, passes=2)[:, 0])
+
+        def store_first(queue, half, y_half, copies):
             queue.dma_start(
                 out=out_rows[:, 0, 0:copies, half * WH : (half + 1) * WH],
                 in_=y_half.unsqueeze(1).to_broadcast([P, copies, WH]),
@@ -284,8 +286,9 @@ def tile_conditionalfeaturesupsample_w4_kernel(
         quantize_up(0, 0, 2)
         quantize_up(0, 2, 3)
         quantize_up(0, 3, 4)
-        first_layer(0, y_first[:], R, nc.scalar)
+        first_layer(0, y_first[:])
         second_layer(0)
+        store_first(nc.scalar, 0, y_first[:], R)
         for k in range(ROW_TAPS):
             weave(k)
         for k in range(ROW_TAPS, KS):
@@ -293,7 +296,8 @@ def tile_conditionalfeaturesupsample_w4_kernel(
         quantize_up(1, 0, 2)
         quantize_up(1, 2, 3)
         quantize_up(1, 3, 4)
-        first_layer(1, y_joined[:, 0:WH], R - 1, nc.sync)
+        first_layer(1, y_joined[:, 0:WH])
+        store_first(nc.sync, 1, y_joined[:, 0:WH], R - 1)
         repeat_second(0)
         second_layer(1)
         repeat_second(1)

@@ -108,12 +108,14 @@ def tile_conditionalfeaturesupsample_w4_kernel(
             src = raw[c][:].rearrange("p j (m t k) -> p t m j k", t=T, k=KS)
             dst = grouped_v[:, :, :, starts[c] : starts[c] + count, :].rearrange("p k t m j -> p t m j k")
             if c < len(CHUNKS) - 1:
+                src_taps = src.rearrange("p t m j (h k) -> p t h m j k", h=2)
+                dst_taps = dst.rearrange("p t m j (h k) -> p t h m j k", h=2)
                 for t in range(vector_slots):
-                    nc.vector.tensor_copy(out=dst[:, t], in_=src[:, t])
+                    nc.vector.tensor_copy(out=dst_taps[:, t], in_=src_taps[:, t])
                     if between and t == 0:
                         between()
                 for t in range(vector_slots, T):
-                    nc.scalar.copy(out=dst[:, t], in_=src[:, t])
+                    nc.scalar.copy(out=dst_taps[:, t], in_=src_taps[:, t])
             else:
                 nc.vector.tensor_copy(out=dst[:, 0, :, :, 0:2], in_=src[:, 0, :, :, 0:2])
                 nc.vector.tensor_copy(out=dst[:, 0, :, :, 2:KS], in_=src[:, 0, :, :, 2:KS])

from contextlib import ExitStack

import concourse.mybir as mybir
from concourse.masks import make_identity

P = 128
C = 512
L = 128
KS = 4
T = 4
NL = 24
R = 4
HALVES = 2
LH = L // HALVES
WH = LH * KS
W = L * KS

F32 = mybir.dt.float32
BF16 = mybir.dt.bfloat16
I32 = mybir.dt.int32
U32 = mybir.dt.uint32
U8 = mybir.dt.uint8
FP8 = mybir.dt.float8_e4m3fn
FP8X4 = mybir.dt.float8_e4m3fn_x4
FP4X4 = mybir.dt.float4_e2m1fn_x4
ADD = mybir.AluOpType.add
MULT = mybir.AluOpType.mult
IDENTITY = mybir.ActivationFunctionType.Identity

FLOPS = 2 * (L * C * C * KS + NL * 128 * C * W)

CHUNKS = ((32, 2), (32, 2), (32, 2), (32, 2))
SPLIT = 16
B1_ROWS = 8
B1_SIDE = NL // B1_ROWS
ROW_TAPS = 2
WARM = (0, 1, 1, 1)
GROUPS = (2, 5, 7, 8)


def tile_conditionalfeaturesupsample_w4_kernel(
    tc, features_bytes, features_scale, wt, bt, w1_words, w1_scales, b1, out
):
    nc = tc.nc
    with ExitStack() as ctx:
        keep = ctx.enter_context(tc.tile_pool(name="keep", bufs=1))
        psum = ctx.enter_context(tc.psum_pool(name="psum", bufs=7))
        ctx.enter_context(tc.manual_schedule())

        x_bytes = keep.tile([P, C], U8, align_bytes=256)
        nc.sync.dma_start(out=x_bytes[:], in_=features_bytes.rearrange("b l c -> (b l) c"))
        x_scale = keep.tile([P, T], F32)

        b1_rows = keep.tile([P, B1_SIDE, 128], BF16, align_bytes=256)
        nc.vector.memset(b1_rows[0:64], 0.0)

        wt_rows = wt.rearrange("(p j) o k -> p j (o k)", j=T)
        raw = []
        starts = []
        m0 = 0
        for c, (count, vector_slots) in enumerate(CHUNKS):
            raw_c = keep.tile([P, T, count * T * KS], BF16, align_bytes=256, tag=f"raw_{c}")
            nc.sync.dma_start(out=raw_c[:], in_=wt_rows[:, :, m0 * T * KS : (m0 + count) * T * KS])
            if c == 0:
                nc.sync.dma_start(out=x_scale[:], in_=features_scale.rearrange("a b (p t) -> p (a b t)", t=T))
            raw.append(raw_c)
            starts.append(m0)
            m0 += count
        bt_sb = keep.tile([P, T], BF16)
        nc.sync.dma_start(out=bt_sb[:], in_=bt.rearrange("(p t) -> p t", t=T))
        nc.sync.dma_start(out=b1_rows[0:B1_ROWS], in_=b1.rearrange("(q i j) -> q i j", i=B1_SIDE, j=128))

        ident = keep.tile([P, P], BF16)
        make_identity(nc, ident[:])
        w1_codes = keep.tile([P, 256 * NL], U8, align_bytes=256)
        w1_plane = keep.tile([P, 128 * NL], U8, align_bytes=256)
        nc.vector.memset(w1_plane[:].bitcast(I32), 0)
        nc.scalar.activation(
            out=b1_rows[64:P], in_=ident[64:P, :].unsqueeze(1).to_broadcast([64, B1_SIDE, P]), func=IDENTITY, scale=0.0
        )

        scale_rows = w1_scales.rearrange("g q n -> (g q) n").bitcast(I32)
        for quad in range(4):
            nc.sync.dma_start(
                out=w1_plane[32 * quad : 32 * quad + 4, :].bitcast(I32), in_=scale_rows[4 * quad : 4 * quad + 4, :]
            )
        nc.sync.dma_start(out=w1_codes[:].bitcast(I32), in_=w1_words.rearrange("g p n -> (g p) n").bitcast(I32))

        x_wide = keep.tile([P, C], BF16, align_bytes=64)
        nc.vector.tensor_copy(out=x_wide[:], in_=x_bytes[:].bitcast(FP8))
        turned = psum.tile([P, T, L], BF16, tag="turn", bufs=1)
        for t in range(T):
            nc.tensor.transpose(turned[:, t, :], x_wide[:, t::T], ident[:])

        x_grouped = keep.tile([P, L, T], BF16, align_bytes=64)
        x_codes = keep.tile([P, L], U32, align_bytes=64)
        x_scales = keep.tile([P, L], U8, align_bytes=64)

        grouped = keep.tile([P, KS * T * P * T], BF16, align_bytes=256, tag="shared")
        grouped_v = grouped[:].rearrange("p (k t m j) -> p k t m j", k=KS, t=T, m=P)
        w_codes = keep.tile([P, KS * T * P], U32, align_bytes=64)
        w_scales = keep.tile([P, KS * T * P], U8, align_bytes=64)

        warm = psum.tile([P, 256], F32, tag="acc")

        def interleave(c, between=None):
            count, vector_slots = CHUNKS[c]
            src = raw[c][:].rearrange("p j (m t k) -> p t m j k", t=T, k=KS)
            dst = grouped_v[:, :, :, starts[c] : starts[c] + count, :].rearrange("p k t m j -> p t m j k")
            if c < len(CHUNKS) - 1:
                src_taps = src.rearrange("p t m j (h k) -> p t h m j k", h=2)
                dst_taps = dst.rearrange("p t m j (h k) -> p t h m j k", h=2)
                for t in range(vector_slots):
                    nc.vector.tensor_copy(out=dst_taps[:, t], in_=src_taps[:, t])
                    if between and t == 0:
                        between()
                for t in range(vector_slots, T):
                    nc.scalar.copy(out=dst_taps[:, t], in_=src_taps[:, t])
            else:
                nc.vector.tensor_copy(out=dst[:, 0, :, :, 0:2], in_=src[:, 0, :, :, 0:2])
                nc.vector.tensor_copy(out=dst[:, 0, :, :, 2:KS], in_=src[:, 0, :, :, 2:KS])
                nc.vector.tensor_copy(out=dst[:, 1, :SPLIT], in_=src[:, 1, :SPLIT])
                src_pair = src[:, 2:T].rearrange("p t m j k -> p m j t k")
                dst_pair = dst[:, 2:T].rearrange("p t m j k -> p m j t k")
                nc.scalar.copy(out=dst_pair[:, :, :, :, 0:2], in_=src_pair[:, :, :, :, 0:2])
                nc.scalar.copy(out=dst[:, 1, SPLIT:], in_=src[:, 1, SPLIT:])
                for k in (2, 3):
                    nc.scalar.copy(out=dst_pair[:, :, :, :, k], in_=src_pair[:, :, :, :, k])
            for i in range(WARM[c]):
                words = raw[c][:].rearrange("p j n -> p (j n)").bitcast(F32)
                nc.tensor.matmul(warm[:], lhsT=words[:, 0:P], rhs=words[:, 0:256], start=True, stop=True)

        def quantize_w(k, t, half):
            c0 = (k * T + t) * P + half * 64
            nc.vector.quantize_mx(
                out=w_codes[:, c0 : c0 + 64].bitcast(FP8X4),
                scales=w_scales[:, c0 : c0 + 64],
                in_=grouped[:, T * c0 : T * (c0 + 64)],
            )

        def scale_x():
            nc.vector.tensor_tensor(
                out=x_grouped[:],
                in0=turned[:].rearrange("p t l -> p l t"),
                in1=x_scale[:].unsqueeze(1).to_broadcast([P, L, T]),
                op=MULT,
            )

        def quantize_x():
            nc.vector.quantize_mx(
                out=x_codes[:].bitcast(FP8X4), scales=x_scales[:], in_=x_grouped[:].rearrange("p l t -> p (l t)")
            )

        second_half = [c for c in range(len(CHUNKS)) if starts[c] >= 64]
        interleave(0, between=scale_x)
        quantize_x()
        interleave(1)
        for t in range(T):
            for k in range(KS):
                quantize_w(k, t, 0)
        for c in second_half:
            interleave(c)

        up_grouped = keep.tile([P, HALVES, KS, LH, T], BF16, align_bytes=64)
        up_codes = keep.tile([P, W], U32, align_bytes=64)
        up_scales = keep.tile([P, W], U8, align_bytes=64)
        up_acc = []
        for k in range(KS):
            acc_k = psum.tile([P, T, L], F32, tag="acc")
            up_acc.append(acc_k)

        def finish_w(k, t):
            quantize_w(k, t, 1)
            c0 = (k * T + t) * P
            nc.tensor.matmul_mx(
                out=up_acc[k][:, t, :],
                lhsT=w_codes[:, c0 : c0 + P].bitcast(FP8X4),
                lhsT_scale=w_scales[:, c0 : c0 + P],
                rhs=x_codes[:].bitcast(FP8X4),
                rhs_scale=x_scales[:],
                start=True,
                stop=True,
            )

        def add_bias(k, half):
            nc.vector.tensor_tensor(
                out=up_grouped[:, half, k],
                in0=up_acc[k][:, :, half * LH : (half + 1) * LH].rearrange("p t l -> p l t"),
                in1=bt_sb[:].unsqueeze(1).to_broadcast([P, LH, T]),
                op=ADD,
            )

        def add_bias_scalar(k, half):
            for t in range(T):
                nc.scalar.activation(
                    out=up_grouped[:, half, k, :, t],
                    in_=up_acc[k][:, t, half * LH : (half + 1) * LH],
                    func=IDENTITY,
                    bias=bt_sb[:, t : t + 1],
                )

        up_rows = []
        for k in range(ROW_TAPS):
            rows_k = keep.tile([P, T, LH], BF16, align_bytes=64, tag=f"up_rows_{k}")
            up_rows.append(rows_k)

        def empty_rows(k):
            for t in range(T):
                nc.scalar.activation(
                    out=up_rows[k][:, t, :], in_=up_acc[k][:, t, LH:L], func=IDENTITY, bias=bt_sb[:, t : t + 1]
                )

        def weave(k):
            nc.vector.tensor_copy(
                out=up_grouped[:, 1, k].rearrange("p (c i) t -> p c t i", i=4),
                in_=up_rows[k][:].rearrange("p t (c i) -> p c t i", i=4),
            )

        def quantize_up(half, k0, k1):
            cols = slice(half * WH + k0 * LH, half * WH + k1 * LH)
            nc.vector.quantize_mx(
                out=up_codes[:, cols].bitcast(FP8X4),
                scales=up_scales[:, cols],
                in_=up_grouped[:, half, k0:k1].rearrange("p k l t -> p (k l t)"),
            )

        for k, t in ((0, 0), (0, 2), (0, 3), (1, 0), (0, 1), (1, 1), (1, 2), (1, 3)):
            finish_w(k, t)
        for slots in ((0, 1), (2, 3)):
            for k in (2, 3):
                for t in slots:
                    finish_w(k, t)

        b1_turned = psum.tile([P, B1_SIDE, B1_ROWS], F32, tag="acc")
        for i in range(B1_SIDE):
            nc.tensor.matmul(b1_turned[:, i, :], lhsT=b1_rows[:, i, :], rhs=ident[:, 0:B1_ROWS], start=True, stop=True)
        b1_cols = keep.tile([P, B1_ROWS, B1_SIDE], F32)

        out_rows = out.rearrange("j b n (r w) -> j (b n) r w", r=R)

        def multiply(n, h0, h1, passes=1):
            acc = psum.tile([P, h1 - h0, KS, LH], F32, tag="acc")
            width = (h1 - h0) * WH // passes
            for c0 in range(0, (h1 - h0) * WH, width):
                cols = slice(h0 * WH + c0, h0 * WH + c0 + width)
                nc.tensor.matmul_mx(
                    out=acc[:].rearrange("p h k l -> p (h k l)")[:, c0 : c0 + width],
                    lhsT=w1_codes[:, 256 * n : 256 * (n + 1)].bitcast(FP4X4),
                    lhsT_scale=w1_plane[:, 128 * n : 128 * (n + 1)],
                    rhs=up_codes[:, cols].bitcast(FP8X4),
                    rhs_scale=up_scales[:, cols],
                    start=True,
                    stop=True,
                )
            return acc[:].rearrange("p h k l -> p h l k")

        def empty_scalar(n, dst, src):
            nc.scalar.activation(out=dst, in_=src, func=IDENTITY, bias=b1_cols[:].rearrange("p q i -> p (q i)")[:, n : n + 1])

        y_first = keep.tile([P, WH], F32, align_bytes=256)
        y_joined = keep.tile([P, WH + R * W], F32, align_bytes=256)
        y_second = y_joined[:, WH:].rearrange("p (r h l k) -> p r h l k", r=R, h=HALVES, k=KS)

        def first_layer(half, y_half):
            empty_scalar(0, y_half.rearrange("p (l k) -> p l k", k=KS), multiply(0, half, half + 1, passes=2)[:, 0])

        def store_first(queue, half, y_half, copies):
            queue.dma_start(
                out=out_rows[:, 0, 0:copies, half * WH : (half + 1) * WH],
                in_=y_half.unsqueeze(1).to_broadcast([P, copies, WH]),
            )

        def second_layer(half):
            empty_scalar(1, y_second[:, 0, half], multiply(1, half, half + 1)[:, 0])

        def repeat_second(half):
            halves = y_second.rearrange("p r h (a l) k -> p h a r (l k)", a=2)
            nc.vector.tensor_copy(
                out=halves[:, half, :, 1:R], in_=halves[:, half, :, 0:1].to_broadcast([P, 2, R - 1, WH // 2])
            )

        add_bias_scalar(0, 0)
        for k in range(1, KS):
            add_bias(k, 0)
        for k in range(ROW_TAPS):
            empty_rows(k)
        nc.scalar.copy(out=b1_cols[:], in_=b1_turned[:].rearrange("p i q -> p q i"))
        quantize_up(0, 0, 2)
        quantize_up(0, 2, 3)
        quantize_up(0, 3, 4)
        first_layer(0, y_first[:])
        second_layer(0)
        store_first(nc.scalar, 0, y_first[:], R)
        for k in range(ROW_TAPS):
            weave(k)
        for k in range(ROW_TAPS, KS):
            add_bias(k, 1)
        quantize_up(1, 0, 2)
        quantize_up(1, 2, 3)
        quantize_up(1, 3, 4)
        first_layer(1, y_joined[:, 0:WH])
        store_first(nc.sync, 1, y_joined[:, 0:WH], R - 1)
        repeat_second(0)
        second_layer(1)
        repeat_second(1)
        nc.sync.dma_start(out=out.rearrange("j b n w -> j (b n w)")[:, R * W - WH : 2 * R * W], in_=y_joined[:])

        n = 2
        for size in GROUPS:
            y_group = keep.tile([P, size, R, W], F32, align_bytes=256, tag="shared" if n == 2 else f"y_group_{n}")
            for i in range(size):
                first_copy = y_group[:, i, 0, :]
                empty_scalar(n + i, first_copy.rearrange("p (h l k) -> p h l k", h=HALVES, k=KS), multiply(n + i, 0, HALVES))
                nc.vector.tensor_copy(
                    out=y_group[:, i, 1:R, :].rearrange("p r (h w) -> p h r w", h=HALVES),
                    in_=first_copy.rearrange("p (h w) -> p h w", h=HALVES).unsqueeze(2).to_broadcast([P, HALVES, R - 1, WH]),
                )
            nc.sync.dma_start(out=out_rows[:, n : n + size], in_=y_group[:])
            n += size
